import numpy as np
import ml_dtypes


def mxq(x, axis, fmt="e4m3"):
    dtype, down = {"e4m3": (ml_dtypes.float8_e4m3fn, 7), "e5m2": (ml_dtypes.float8_e5m2, 14)}[fmt]
    v = np.moveaxis(np.asarray(x, np.float32).astype(ml_dtypes.bfloat16).astype(np.float64), axis, -1)
    blocks = v.reshape(v.shape[:-1] + (-1, 32))
    amax = np.abs(blocks).max(-1, keepdims=True)
    byte = np.maximum(np.where(amax > 0, np.frexp(amax)[1] - 1 + 127, 0) - down, 1)
    scale = np.exp2(byte - 127.0)
    codes = (blocks / scale).astype(np.float32).astype(dtype).astype(np.float64)
    return np.moveaxis((codes * scale).reshape(v.shape), -1, axis)


WIDE = False


def mx_kscale(k):
    if not WIDE:
        return np.ones(k)
    levels = np.array([10, -10, 5, -5, 0])
    a = np.random.permutation(np.resize(levels, k // 512 * 4)).reshape(k // 512, 4)
    idx = np.arange(k)
    return np.exp2(a[idx // 512, idx % 128 // 32])


BF16 = ml_dtypes.bfloat16


def bf(x):
    return np.asarray(x, np.float32).astype(BF16)


def f64(x):
    return np.asarray(x).astype(np.float64)


B, L, D_G, D_SP, H, OUT = 1, 128, 512, 512, 512, 128


def softmax1(m):
    e = np.exp(m - m.max())
    return e / e.sum()


def setup_inputs():
    s, u = mx_kscale(D_G), mx_kscale(D_SP)
    s2, u2 = np.concatenate([s, s])[:, None], np.concatenate([u, u])[:, None]
    mix0 = np.array([0.4, -0.4])
    return {
        "global_outputs": bf(np.random.standard_normal((B, L, D_G)) * s),
        "sp_outputs": bf(np.random.standard_normal((B, L, D_SP)) * u),
        "W_utt": bf(np.random.standard_normal((D_G + D_G, H)) * 0.5 / np.sqrt(D_G) / s2),
        "b_utt": bf(np.random.standard_normal(H) * 0.3),
        "W_sp": bf(np.random.standard_normal((D_SP + D_SP, H)) * 0.5 / np.sqrt(D_SP) / u2),
        "b_sp": bf(np.random.standard_normal(H) * 0.3),
        "W2": bf(np.random.standard_normal((H, OUT)) * 1.5 / np.sqrt(H)),
        "b2": bf(np.random.standard_normal(OUT) * 0.3),
        "mix_w": bf(mix0 + 0.1 * np.random.standard_normal(mix0.shape)),
        "gamma": bf(np.atleast_1d(1.5 + 0.1 * np.random.standard_normal())),
    }


def reference(global_outputs, sp_outputs, W_utt, b_utt, W_sp, b_sp, W2, b2, mix_w, gamma):
    gq = mxq(f64(global_outputs), 2, "e4m3")
    wu = f64(W_utt)
    g_j = gq @ mxq(wu[:D_G], 0, "e4m3")
    g_i = gq @ mxq(wu[D_G:], 0, "e4m3")
    utt_hidden = np.tanh(g_j[:, None, :, :] + g_i[:, :, None, :] + f64(b_utt))

    sq = mxq(f64(sp_outputs), 2, "e4m3")
    ws = f64(W_sp)
    s_j = sq @ mxq(ws[:D_SP], 0, "e4m3")
    s_i = sq @ mxq(ws[D_SP:], 0, "e4m3")
    sp_hidden = np.tanh(s_j[:, None, :, :] + s_i[:, :, None, :] + f64(b_sp))

    w = softmax1(f64(mix_w))
    state_hidden = f64(gamma) * (w[0] * utt_hidden + w[1] * sp_hidden)

    return np.tanh((mxq(state_hidden, 3, "e4m3") @ mxq(f64(W2), 0, "e4m3")) + f64(b2))

@@ -1,0 +1,218 @@
+from contextlib import ExitStack
+
+import concourse.bass as bass
+import concourse.mybir as mybir
+import concourse.tile as tile
+from concourse.masks import make_identity
+
+F32 = mybir.dt.float32
+BF16 = mybir.dt.bfloat16
+U32 = mybir.dt.uint32
+U8 = mybir.dt.uint8
+FP8X4 = mybir.dt.float8_e4m3fn_x4
+AF = mybir.ActivationFunctionType
+ALU = mybir.AluOpType
+AX = mybir.AxisListType
+
+P = 128
+L = 128
+D = 512
+H = 512
+OUT = 128
+PACK = 4
+JR = 4
+ROUNDS = L // JR
+COLS = JR * L
+
+FLOPS = 4 * 2 * L * D * H + 2 * L * L * H * OUT
+
+
+def tile_stateencoder_pa_t_kernel(
+    tc, global_outputs, sp_outputs, W_utt, b_utt, W_sp, b_sp, W2, b2, mix_w, gamma, out
+):
+    nc = tc.nc
+    acts = [global_outputs, sp_outputs]
+    weights = [W_utt, W_sp]
+    out_rows = out.rearrange("b i j o -> (b i) j o")
+
+    with ExitStack() as ctx:
+        const = ctx.enter_context(tc.tile_pool(name="const", bufs=1))
+        xpool = ctx.enter_context(tc.tile_pool(name="xpool", bufs=3))
+        gpool = ctx.enter_context(tc.tile_pool(name="gpool", bufs=2))
+        qpool = ctx.enter_context(tc.tile_pool(name="qpool", bufs=3))
+        ypool = ctx.enter_context(tc.tile_pool(name="ypool", bufs=4))
+        psum = ctx.enter_context(tc.psum_pool(name="psum", bufs=8))
+
+        warm = const.tile([P, 1], F32, name="warm")
+        nc.vector.memset(warm[:], 0.0)
+        nc.scalar.activation(out=warm[:], in_=warm[:], func=AF.Exp)
+        rowz = const.tile([P, 256], BF16, name="rowz")
+        nc.vector.memset(rowz[:], 0.0)
+        brow = const.tile([P, P], BF16, name="brow")
+        nc.vector.memset(brow[:], 0.0)
+        sel = const.tile([P, P], BF16, name="sel")
+        nc.vector.memset(sel[:], 0.0)
+        nc.vector.memset(sel[0:1, :], 1.0)
+        ident = const.tile([P, P], BF16, name="ident")
+        make_identity(nc, ident[:])
+
+        nc.scalar.dma_start(out=brow[0:4, :], in_=b_utt.rearrange("(t p) -> t p", t=PACK))
+        nc.scalar.dma_start(out=brow[4:8, :], in_=b_sp.rearrange("(t p) -> t p", t=PACK))
+        nc.scalar.dma_start(out=rowz[0:1, 0:OUT], in_=b2.rearrange("(x o) -> x o", x=1))
+        nc.scalar.dma_start(out=rowz[0:1, 128:130], in_=mix_w.rearrange("(x o) -> x o", x=1))
+        nc.scalar.dma_start(out=rowz[0:1, 144:145], in_=gamma.rearrange("(x o) -> x o", x=1))
+
+        a_sb = []
+        w_raw = []
+        for s in range(2):
+            a_t = const.tile([P, D], BF16, name="a_sb%d" % s)
+            nc.sync.dma_start(out=a_t[:], in_=acts[s].rearrange("b l k -> (b l) k"))
+            a_sb.append(a_t)
+            w_t = const.tile([P, 2, PACK, H], BF16, name="w_raw%d" % s)
+            for a in range(2):
+                nc.sync.dma_start(
+                    out=w_t[:, a],
+                    in_=weights[s][a * D : (a + 1) * D, :].rearrange("(t p) n -> p t n", t=PACK, p=P),
+                )
+            w_raw.append(w_t)
+        w2_raw = const.tile([P, PACK, OUT], BF16, name="w2_raw")
+        nc.sync.dma_start(out=w2_raw[:], in_=W2.rearrange("(t p) o -> p t o", t=PACK, p=P))
+
+        pb = psum.tile([P, P], BF16, name="pb", tag="ps")
+        nc.tensor.transpose(pb[:], brow[:], ident[:])
+        b_t = const.tile([P, 8], F32, name="b_t")
+        nc.vector.tensor_copy(out=b_t[:], in_=pb[:, 0:8])
+
+        pc = psum.tile([P, 256], F32, name="pc", tag="ps")
+        nc.tensor.matmul(pc[:], lhsT=sel[:], rhs=rowz[:], start=True, stop=True)
+        b2bc = const.tile([P, OUT], F32, name="b2bc")
+        nc.vector.tensor_copy(out=b2bc[:], in_=pc[:, 0:OUT])
+        sm = const.tile([P, 32], F32, name="sm")
+        nc.vector.tensor_copy(out=sm[:], in_=pc[:, 128:160])
+        mx = const.tile([P, 1], F32, name="mx")
+        nc.vector.reduce_max(out=mx[:], in_=sm[:, 0:2], axis=AX.X)
+        nmx = const.tile([P, 1], F32, name="nmx")
+        nc.vector.tensor_scalar(out=nmx[:], in0=mx[:], scalar1=-1.0, scalar2=None, op0=ALU.mult)
+        ex = const.tile([P, 2], F32, name="ex")
+        nc.scalar.activation(out=ex[:], in_=sm[:, 0:2], func=AF.Exp, bias=nmx[:, 0:1], scale=1.0)
+        ssum = const.tile([P, 1], F32, name="ssum")
+        nc.vector.reduce_sum(out=ssum[:], in_=ex[:], axis=AX.X)
+        rsum = const.tile([P, 1], F32, name="rsum")
+        nc.vector.reciprocal(out=rsum[:], in_=ssum[:])
+        cc = const.tile([P, 2], F32, name="cc")
+        nc.vector.tensor_scalar(
+            out=cc[:], in0=ex[:], scalar1=rsum[:, 0:1], scalar2=sm[:, 16:17], op0=ALU.mult, op1=ALU.mult
+        )
+
+        gi_t = []
+        gjb = []
+        for s in range(2):
+            pt = psum.tile([P, PACK, L], BF16, name="pt", tag="ps")
+            for t in range(PACK):
+                nc.tensor.transpose(pt[:, t, :], a_sb[s][:, t * P : (t + 1) * P], ident[:])
+            a_grp = const.tile([P, L, PACK], BF16, name="a_grp%d" % s, align_bytes=64)
+            nc.vector.tensor_copy(out=a_grp[:], in_=pt[:].rearrange("p t l -> p l t"))
+            w_grp = []
+            for a in range(2):
+                wg = const.tile([P, H, PACK], BF16, name="w_grp%d%d" % (s, a), align_bytes=64)
+                nc.vector.tensor_copy(
+                    out=wg[:].rearrange("p (c i) t -> p c t i", i=4),
+                    in_=w_raw[s][:, a].rearrange("p t (c i) -> p c t i", i=4),
+                )
+                w_grp.append(wg)
+            a_c = const.tile([P, L], U32, name="a_c%d" % s, align_bytes=64)
+            a_s = const.tile([P, L], U8, name="a_s%d" % s, align_bytes=64)
+            nc.vector.quantize_mx(
+                out=a_c[:].bitcast(FP8X4), scales=a_s[:], in_=a_grp[:].rearrange("p l t -> p (l t)")
+            )
+            for a in range(2):
+                w_c = const.tile([P, H], U32, name="w_c%d%d" % (s, a), align_bytes=64)
+                w_s = const.tile([P, H], U8, name="w_s%d%d" % (s, a), align_bytes=64)
+                nc.vector.quantize_mx(
+                    out=w_c[:].bitcast(FP8X4), scales=w_s[:], in_=w_grp[a][:].rearrange("p c t -> p (c t)")
+                )
+                pg = psum.tile([P, PACK, L], F32, name="pg", tag="ps")
+                for t in range(PACK):
+                    cols = slice(t * P, (t + 1) * P)
+                    nc.tensor.matmul_mx(
+                        out=pg[:, t, :],
+                        lhsT=w_c[:, cols].bitcast(FP8X4),
+                        lhsT_scale=w_s[:, cols],
+                        rhs=a_c[:].bitcast(FP8X4),
+                        rhs_scale=a_s[:],
+                        start=True,
+                        stop=True,
+                    )
+                if a == 0:
+                    g = const.tile([P, PACK, L], F32, name="gjb%d" % s)
+                    nc.vector.tensor_tensor(
+                        out=g[:],
+                        in0=pg[:],
+                        in1=b_t[:, PACK * s : PACK * (s + 1)].unsqueeze(2).to_broadcast([P, PACK, L]),
+                        op=ALU.add,
+                    )
+                    gjb.append(g)
+                else:
+                    g = const.tile([P, PACK, L], F32, name="gi_t%d" % s)
+                    nc.scalar.copy(out=g[:], in_=pg[:])
+                    gi_t.append(g)
+
+        w2_grp = const.tile([P, OUT, PACK], BF16, name="w2_grp", align_bytes=64)
+        nc.vector.tensor_copy(out=w2_grp[:], in_=w2_raw[:].rearrange("p t o -> p o t"))
+        w2_c = const.tile([P, OUT], U32, name="w2_c", align_bytes=64)
+        w2_s = const.tile([P, OUT], U8, name="w2_s", align_bytes=64)
+        nc.vector.quantize_mx(
+            out=w2_c[:].bitcast(FP8X4), scales=w2_s[:], in_=w2_grp[:].rearrange("p o t -> p (o t)")
+        )
+
+        for r in range(ROUNDS):
+            xs = []
+            for s in range(2):
+                x = xpool.tile([P, PACK, COLS], F32, name="x%d" % s)
+                for jl in range(JR):
+                    j = r * JR + jl
+                    for t in range(PACK):
+                        nc.scalar.activation(
+                            out=x[:, t, jl * L : (jl + 1) * L],
+                            in_=gi_t[s][:, t, :],
+                            func=AF.Tanh,
+                            bias=gjb[s][:, t, j : j + 1],
+                            scale=1.0,
+                        )
+                xs.append(x)
+                if s == 0:
+                    nc.vector.tensor_scalar(
+                        out=x[:], in0=x[:], scalar1=cc[:, 0:1], scalar2=None, op0=ALU.mult
+                    )
+            grp = gpool.tile([P, COLS, PACK], BF16, name="grp", align_bytes=64)
+            nc.vector.scalar_tensor_tensor(
+                out=grp[:],
+                in0=xs[1][:].rearrange("p t c -> p c t"),
+                scalar=cc[:, 1:2],
+                in1=xs[0][:].rearrange("p t c -> p c t"),
+                op0=ALU.mult,
+                op1=ALU.add,
+            )
+            s_c = qpool.tile([P, COLS], U32, name="s_c", align_bytes=64)
+            s_s = qpool.tile([P, COLS], U8, name="s_s", align_bytes=64)
+            nc.vector.quantize_mx(
+                out=s_c[:].bitcast(FP8X4), scales=s_s[:], in_=grp[:].rearrange("p c t -> p (c t)")
+            )
+            po = psum.tile([P, JR, OUT], F32, name="po", tag="ps")
+            for jl in range(JR):
+                cols = slice(jl * L, (jl + 1) * L)
+                nc.tensor.matmul_mx(
+                    out=po[:, jl, :],
+                    lhsT=s_c[:, cols].bitcast(FP8X4),
+                    lhsT_scale=s_s[:, cols],
+                    rhs=w2_c[:].bitcast(FP8X4),
+                    rhs_scale=w2_s[:],
+                    start=True,
+                    stop=True,
+                )
+            y = ypool.tile([P, JR, OUT], F32, name="y")
+            nc.vector.tensor_tensor(
+                out=y[:], in0=po[:], in1=b2bc[:].unsqueeze(1).to_broadcast([P, JR, OUT]), op=ALU.add
+            )
+            nc.scalar.activation(out=y[:], in_=y[:], func=AF.Tanh)
+            nc.sync.dma_start(out=out_rows[:, r * JR : (r + 1) * JR, :], in_=y[:])

@@ -23,6 +23,9 @@ PACK = 4
 JR = 4
 ROUNDS = L // JR
 COLS = JR * L
+FIRST_HELD = ROUNDS - 6
+
+RHO_MAX = 2.0**60
 
 FLOPS = 4 * 2 * L * D * H + 2 * L * L * H * OUT
 
@@ -40,7 +43,7 @@ def tile_stateencoder_pa_t_kernel(
         xpool = ctx.enter_context(tc.tile_pool(name="xpool", bufs=3))
         gpool = ctx.enter_context(tc.tile_pool(name="gpool", bufs=2))
         qpool = ctx.enter_context(tc.tile_pool(name="qpool", bufs=3))
-        ypool = ctx.enter_context(tc.tile_pool(name="ypool", bufs=4))
+        ypool = ctx.enter_context(tc.tile_pool(name="ypool", bufs=8))
         psum = ctx.enter_context(tc.psum_pool(name="psum", bufs=8))
 
         warm = const.tile([P, 1], F32, name="warm")
@@ -89,20 +92,18 @@ def tile_stateencoder_pa_t_kernel(
         nc.vector.tensor_copy(out=b2bc[:], in_=pc[:, 0:OUT])
         sm = const.tile([P, 32], F32, name="sm")
         nc.vector.tensor_copy(out=sm[:], in_=pc[:, 128:160])
-        mx = const.tile([P, 1], F32, name="mx")
-        nc.vector.reduce_max(out=mx[:], in_=sm[:, 0:2], axis=AX.X)
-        nmx = const.tile([P, 1], F32, name="nmx")
-        nc.vector.tensor_scalar(out=nmx[:], in0=mx[:], scalar1=-1.0, scalar2=None, op0=ALU.mult)
-        ex = const.tile([P, 2], F32, name="ex")
-        nc.scalar.activation(out=ex[:], in_=sm[:, 0:2], func=AF.Exp, bias=nmx[:, 0:1], scale=1.0)
-        ssum = const.tile([P, 1], F32, name="ssum")
-        nc.vector.reduce_sum(out=ssum[:], in_=ex[:], axis=AX.X)
-        rsum = const.tile([P, 1], F32, name="rsum")
-        nc.vector.reciprocal(out=rsum[:], in_=ssum[:])
-        cc = const.tile([P, 2], F32, name="cc")
-        nc.vector.tensor_scalar(
-            out=cc[:], in0=ex[:], scalar1=rsum[:, 0:1], scalar2=sm[:, 16:17], op0=ALU.mult, op1=ALU.mult
-        )
+        dd = const.tile([P, 1], F32, name="dd")
+        nc.vector.tensor_tensor(out=dd[:], in0=sm[:, 0:1], in1=sm[:, 1:2], op=ALU.subtract)
+        ex = const.tile([P, 1], F32, name="ex")
+        nc.scalar.activation(out=ex[:], in_=dd[:], func=AF.Exp)
+        rho = const.tile([P, 1], F32, name="rho")
+        nc.vector.tensor_scalar(out=rho[:], in0=ex[:], scalar1=RHO_MAX, scalar2=None, op0=ALU.min)
+        den = const.tile([P, 1], F32, name="den")
+        nc.vector.tensor_scalar(out=den[:], in0=rho[:], scalar1=1.0, scalar2=None, op0=ALU.add)
+        rden = const.tile([P, 1], F32, name="rden")
+        nc.vector.reciprocal(out=rden[:], in_=den[:])
+        kap = const.tile([P, 1], F32, name="kap")
+        nc.vector.tensor_tensor(out=kap[:], in0=rden[:], in1=sm[:, 16:17], op=ALU.mult)
 
         gi_t = []
         gjb = []
@@ -154,7 +155,10 @@ def tile_stateencoder_pa_t_kernel(
                     gjb.append(g)
                 else:
                     g = const.tile([P, PACK, L], F32, name="gi_t%d" % s)
-                    nc.scalar.copy(out=g[:], in_=pg[:])
+                    if s == 0:
+                        nc.scalar.copy(out=g[:], in_=pg[:])
+                    else:
+                        nc.vector.tensor_copy(out=g[:], in_=pg[:])
                     gi_t.append(g)
 
         w2_grp = const.tile([P, OUT, PACK], BF16, name="w2_grp", align_bytes=64)
@@ -165,44 +169,63 @@ def tile_stateencoder_pa_t_kernel(
             out=w2_c[:].bitcast(FP8X4), scales=w2_s[:], in_=w2_grp[:].rearrange("p o t -> p (o t)")
         )
 
-        for r in range(ROUNDS):
-            xs = []
-            for s in range(2):
-                x = xpool.tile([P, PACK, COLS], F32, name="x%d" % s)
-                for jl in range(JR):
-                    j = r * JR + jl
-                    for t in range(PACK):
-                        nc.scalar.activation(
-                            out=x[:, t, jl * L : (jl + 1) * L],
-                            in_=gi_t[s][:, t, :],
-                            func=AF.Tanh,
-                            bias=gjb[s][:, t, j : j + 1],
-                            scale=1.0,
-                        )
-                xs.append(x)
-                if s == 0:
-                    nc.vector.tensor_scalar(
-                        out=x[:], in0=x[:], scalar1=cc[:, 0:1], scalar2=None, op0=ALU.mult
+        xs = {}
+        grps = {}
+        codes = {}
+        pos = {}
+        ys = {}
+
+        def tanh1(r, s, jls):
+            if (r, s) not in xs:
+                xs[(r, s)] = xpool.tile([P, PACK, COLS], F32, name="x%d" % s)
+            x = xs[(r, s)]
+            for jl in jls:
+                j = r * JR + jl
+                for t in range(PACK):
+                    nc.scalar.activation(
+                        out=x[:, t, jl * L : (jl + 1) * L],
+                        in_=gi_t[s][:, t, :],
+                        func=AF.Tanh,
+                        bias=gjb[s][:, t, j : j + 1],
+                        scale=1.0,
                     )
-            grp = gpool.tile([P, COLS, PACK], BF16, name="grp", align_bytes=64)
+
+        def mix(r, lo, hi):
+            if r not in grps:
+                grps[r] = gpool.tile([P, COLS, PACK], BF16, name="grp", align_bytes=64)
+            x0 = xs[(r, 0)][:, :, lo * L : hi * L]
+            x1 = xs[(r, 1)][:, :, lo * L : hi * L]
             nc.vector.scalar_tensor_tensor(
-                out=grp[:],
-                in0=xs[1][:].rearrange("p t c -> p c t"),
-                scalar=cc[:, 1:2],
-                in1=xs[0][:].rearrange("p t c -> p c t"),
+                out=x1, in0=x0, scalar=rho[:, 0:1], in1=x1, op0=ALU.mult, op1=ALU.add
+            )
+            nc.vector.tensor_scalar(
+                out=grps[r][:, lo * L : hi * L, :].rearrange("p (c i) t -> p c t i", i=4),
+                in0=x1.rearrange("p t (c i) -> p c t i", i=4),
+                scalar1=kap[:, 0:1],
+                scalar2=None,
                 op0=ALU.mult,
-                op1=ALU.add,
             )
-            s_c = qpool.tile([P, COLS], U32, name="s_c", align_bytes=64)
-            s_s = qpool.tile([P, COLS], U8, name="s_s", align_bytes=64)
+
+        def quant(r, lo, hi):
+            if r not in codes:
+                s_c = qpool.tile([P, COLS], U32, name="s_c", align_bytes=64)
+                s_s = qpool.tile([P, COLS], U8, name="s_s", align_bytes=64)
+                codes[r] = (s_c, s_s)
+            s_c, s_s = codes[r]
             nc.vector.quantize_mx(
-                out=s_c[:].bitcast(FP8X4), scales=s_s[:], in_=grp[:].rearrange("p c t -> p (c t)")
+                out=s_c[:, lo * L : hi * L].bitcast(FP8X4),
+                scales=s_s[:, lo * L : hi * L],
+                in_=grps[r][:, lo * L : hi * L, :].rearrange("p c t -> p (c t)"),
             )
-            po = psum.tile([P, JR, OUT], F32, name="po", tag="ps")
-            for jl in range(JR):
+
+        def stage2(r, lo, hi):
+            if r not in pos:
+                pos[r] = psum.tile([P, JR, OUT], F32, name="po", tag="ps")
+            s_c, s_s = codes[r]
+            for jl in range(lo, hi):
                 cols = slice(jl * L, (jl + 1) * L)
                 nc.tensor.matmul_mx(
-                    out=po[:, jl, :],
+                    out=pos[r][:, jl, :],
                     lhsT=s_c[:, cols].bitcast(FP8X4),
                     lhsT_scale=s_s[:, cols],
                     rhs=w2_c[:].bitcast(FP8X4),
@@ -210,9 +233,59 @@ def tile_stateencoder_pa_t_kernel(
                     start=True,
                     stop=True,
                 )
-            y = ypool.tile([P, JR, OUT], F32, name="y")
+
+        def add_b2(r, lo, hi):
+            if r not in ys:
+                ys[r] = ypool.tile([P, JR, OUT], F32, name="y")
             nc.vector.tensor_tensor(
-                out=y[:], in0=po[:], in1=b2bc[:].unsqueeze(1).to_broadcast([P, JR, OUT]), op=ALU.add
+                out=ys[r][:, lo:hi, :],
+                in0=pos[r][:, lo:hi, :],
+                in1=b2bc[:].unsqueeze(1).to_broadcast([P, hi - lo, OUT]),
+                op=ALU.add,
             )
-            nc.scalar.activation(out=y[:], in_=y[:], func=AF.Tanh)
-            nc.sync.dma_start(out=out_rows[:, r * JR : (r + 1) * JR, :], in_=y[:])
+
+        def tanh2_store(r, lo, hi):
+            y = ys[r][:, lo:hi, :]
+            nc.scalar.activation(out=y, in_=y, func=AF.Tanh)
+            nc.sync.dma_start(out=out_rows[:, r * JR + lo : r * JR + hi, :], in_=y)
+
+        LAST = ROUNDS - 1
+        with tc.manual_schedule():
+            tanh1(0, 0, range(JR))
+            tanh1(1, 0, range(JR))
+            tanh1(0, 1, range(JR))
+            mix(0, 0, JR)
+            tanh1(1, 1, range(JR))
+            quant(0, 0, JR)
+            stage2(0, 0, JR)
+            for r in range(2, LAST):
+                tanh1(r, 0, range(JR))
+                mix(r - 1, 0, JR)
+                add_b2(r - 2, 0, JR)
+                quant(r - 1, 0, JR)
+                stage2(r - 1, 0, JR)
+                tanh1(r, 1, range(JR))
+                if r - 2 < FIRST_HELD:
+                    tanh2_store(r - 2, 0, JR)
+            r = LAST
+            tanh1(r, 0, range(0, 2))
+            tanh1(r, 1, range(0, 2))
+            mix(r - 1, 0, JR)
+            add_b2(r - 2, 0, JR)
+            quant(r - 1, 0, JR)
+            stage2(r - 1, 0, JR)
+            tanh1(r, 0, range(2, 4))
+            tanh1(r, 1, range(2, 4))
+            mix(r, 0, 2)
+            add_b2(r - 1, 0, JR)
+            quant(r, 0, 2)
+            stage2(r, 0, 2)
+            for m in range(FIRST_HELD, LAST):
+                tanh2_store(m, 0, JR)
+            mix(r, 2, 4)
+            add_b2(r, 0, 2)
+            quant(r, 2, 4)
+            stage2(r, 2, 4)
+            tanh2_store(r, 0, 2)
+            add_b2(r, 2, 4)
+            tanh2_store(r, 2, 4)

@@ -1,18 +1,16 @@
 from contextlib import ExitStack
 
-import concourse.bass as bass
 import concourse.mybir as mybir
-import concourse.tile as tile
 from concourse.masks import make_identity
 
 F32 = mybir.dt.float32
 BF16 = mybir.dt.bfloat16
 U32 = mybir.dt.uint32
+I32 = mybir.dt.int32
 U8 = mybir.dt.uint8
 FP8X4 = mybir.dt.float8_e4m3fn_x4
 AF = mybir.ActivationFunctionType
 ALU = mybir.AluOpType
-AX = mybir.AxisListType
 
 P = 128
 L = 128
@@ -20,11 +18,17 @@ D = 512
 H = 512
 OUT = 128
 PACK = 4
-JR = 4
-ROUNDS = L // JR
-COLS = JR * L
+NI = 32
+NJ = 16
+NG = 4
+NQ = NJ // NG
+IBS = L // NI
+JBS = L // NJ
+ROUNDS = IBS * JBS
+COLS = NI * NJ
+HALF = COLS // 2
 FIRST_HELD = ROUNDS - 6
-
+STAGE2_AFTER_BANK = 3
 RHO_MAX = 2.0**60
 
 FLOPS = 4 * 2 * L * D * H + 2 * L * L * H * OUT
@@ -40,11 +44,13 @@ def tile_stateencoder_pa_t_kernel(
 
     with ExitStack() as ctx:
         const = ctx.enter_context(tc.tile_pool(name="const", bufs=1))
+        jpool = ctx.enter_context(tc.tile_pool(name="jpool", bufs=2))
         xpool = ctx.enter_context(tc.tile_pool(name="xpool", bufs=3))
         gpool = ctx.enter_context(tc.tile_pool(name="gpool", bufs=2))
         qpool = ctx.enter_context(tc.tile_pool(name="qpool", bufs=3))
         ypool = ctx.enter_context(tc.tile_pool(name="ypool", bufs=8))
-        psum = ctx.enter_context(tc.psum_pool(name="psum", bufs=8))
+        psx = ctx.enter_context(tc.psum_pool(name="psx", bufs=6))
+        pso = ctx.enter_context(tc.psum_pool(name="pso", bufs=2))
 
         warm = const.tile([P, 1], F32, name="warm")
         nc.vector.memset(warm[:], 0.0)
@@ -58,6 +64,15 @@ def tile_stateencoder_pa_t_kernel(
         nc.vector.memset(sel[0:1, :], 1.0)
         ident = const.tile([P, P], BF16, name="ident")
         make_identity(nc, ident[:])
+        a_s = []
+        a_s4 = []
+        for s in range(2):
+            pl = const.tile([P, L], U8, name="a_s%d" % s, align_bytes=64)
+            nc.vector.memset(pl[:].bitcast(I32), 0)
+            a_s.append(pl)
+            pl4 = const.tile([P, PACK * L], U8, name="a_s4%d" % s, align_bytes=64)
+            nc.vector.memset(pl4[:].bitcast(I32), 0)
+            a_s4.append(pl4)
 
         nc.scalar.dma_start(out=brow[0:4, :], in_=b_utt.rearrange("(t p) -> t p", t=PACK))
         nc.scalar.dma_start(out=brow[4:8, :], in_=b_sp.rearrange("(t p) -> t p", t=PACK))
@@ -81,12 +96,12 @@ def tile_stateencoder_pa_t_kernel(
         w2_raw = const.tile([P, PACK, OUT], BF16, name="w2_raw")
         nc.sync.dma_start(out=w2_raw[:], in_=W2.rearrange("(t p) o -> p t o", t=PACK, p=P))
 
-        pb = psum.tile([P, P], BF16, name="pb", tag="ps")
+        pb = pso.tile([P, P], BF16, name="pb", tag="po")
         nc.tensor.transpose(pb[:], brow[:], ident[:])
         b_t = const.tile([P, 8], F32, name="b_t")
         nc.vector.tensor_copy(out=b_t[:], in_=pb[:, 0:8])
 
-        pc = psum.tile([P, 256], F32, name="pc", tag="ps")
+        pc = pso.tile([P, 256], F32, name="pc", tag="po")
         nc.tensor.matmul(pc[:], lhsT=sel[:], rhs=rowz[:], start=True, stop=True)
         b2bc = const.tile([P, OUT], F32, name="b2bc")
         nc.vector.tensor_copy(out=b2bc[:], in_=pc[:, 0:OUT])
@@ -105,61 +120,93 @@ def tile_stateencoder_pa_t_kernel(
         kap = const.tile([P, 1], F32, name="kap")
         nc.vector.tensor_tensor(out=kap[:], in0=rden[:], in1=sm[:, 16:17], op=ALU.mult)
 
-        gi_t = []
-        gjb = []
+        a_c = []
+        it_c = []
+        it_s = []
+        w_c = []
+        w_s = []
+        jts = {}
+
+        def build_j(s, jb):
+            jt_c = jpool.tile([P, COLS], U32, name="jt_c%d" % s, align_bytes=64)
+            jt_s = jpool.tile([P, COLS], U8, name="jt_s%d" % s, align_bytes=64)
+            js = slice(jb * NJ, (jb + 1) * NJ)
+            nc.vector.tensor_copy(
+                out=jt_c[:].bitcast(I32).rearrange("p (g q l) -> p g q l", g=NG, q=NQ),
+                in_=a_c[s][:]
+                .bitcast(I32)[:, js]
+                .rearrange("p (q g) -> p g q", g=NG)
+                .unsqueeze(3)
+                .to_broadcast([P, NG, NQ, NI]),
+            )
+            nc.vector.tensor_copy(
+                out=jt_s[:].bitcast(I32).rearrange("p (g q w) -> p g q w", g=NG, q=NQ),
+                in_=a_s4[s][:]
+                .bitcast(I32)[:, js]
+                .rearrange("p (q g) -> p g q", g=NG)
+                .unsqueeze(3)
+                .to_broadcast([P, NG, NQ, NI // 4]),
+            )
+            jts[(s, jb)] = (jt_c, jt_s)
+
         for s in range(2):
-            pt = psum.tile([P, PACK, L], BF16, name="pt", tag="ps")
+            pt = psx.tile([P, PACK, L], BF16, name="pt", tag="px")
             for t in range(PACK):
                 nc.tensor.transpose(pt[:, t, :], a_sb[s][:, t * P : (t + 1) * P], ident[:])
             a_grp = const.tile([P, L, PACK], BF16, name="a_grp%d" % s, align_bytes=64)
             nc.vector.tensor_copy(out=a_grp[:], in_=pt[:].rearrange("p t l -> p l t"))
-            w_grp = []
+            a_grp4 = const.tile([P, L, PACK, PACK], BF16, name="a_grp4%d" % s, align_bytes=64)
+            nc.scalar.copy(
+                out=a_grp4[:],
+                in_=a_grp[:].unsqueeze(2).to_broadcast([P, L, PACK, PACK]),
+            )
+            ac = const.tile([P, L], U32, name="a_c%d" % s, align_bytes=64)
+            nc.vector.quantize_mx(
+                out=ac[:].bitcast(FP8X4), scales=a_s[s][:], in_=a_grp[:].rearrange("p l t -> p (l t)")
+            )
+            a_c.append(ac)
+            ac4 = const.tile([P, PACK * L], U32, name="a_c4%d" % s, align_bytes=64)
+            nc.vector.quantize_mx(
+                out=ac4[:].bitcast(FP8X4), scales=a_s4[s][:], in_=a_grp4[:].rearrange("p l r t -> p (l r t)")
+            )
+            ic = const.tile([P, IBS, HALF], U32, name="it_c%d" % s, align_bytes=64)
+            isc = const.tile([P, IBS, HALF], U8, name="it_s%d" % s, align_bytes=64)
+            nc.vector.tensor_copy(
+                out=ic[:].bitcast(I32).rearrange("p b (r l) -> p b r l", l=NI),
+                in_=ac[:]
+                .bitcast(I32)
+                .rearrange("p (b l) -> p b l", b=IBS)
+                .unsqueeze(2)
+                .to_broadcast([P, IBS, HALF // NI, NI]),
+            )
+            nc.vector.tensor_copy(
+                out=isc[:].bitcast(I32).rearrange("p b (r w) -> p b r w", w=NI // 4),
+                in_=a_s[s][:]
+                .bitcast(I32)
+                .rearrange("p (b w) -> p b w", b=IBS)
+                .unsqueeze(2)
+                .to_broadcast([P, IBS, HALF // NI, NI // 4]),
+            )
+            it_c.append(ic)
+            it_s.append(isc)
+            build_j(s, 0)
+            wcs = []
+            wss = []
             for a in range(2):
                 wg = const.tile([P, H, PACK], BF16, name="w_grp%d%d" % (s, a), align_bytes=64)
                 nc.vector.tensor_copy(
                     out=wg[:].rearrange("p (c i) t -> p c t i", i=4),
                     in_=w_raw[s][:, a].rearrange("p t (c i) -> p c t i", i=4),
                 )
-                w_grp.append(wg)
-            a_c = const.tile([P, L], U32, name="a_c%d" % s, align_bytes=64)
-            a_s = const.tile([P, L], U8, name="a_s%d" % s, align_bytes=64)
-            nc.vector.quantize_mx(
-                out=a_c[:].bitcast(FP8X4), scales=a_s[:], in_=a_grp[:].rearrange("p l t -> p (l t)")
-            )
-            for a in range(2):
-                w_c = const.tile([P, H], U32, name="w_c%d%d" % (s, a), align_bytes=64)
-                w_s = const.tile([P, H], U8, name="w_s%d%d" % (s, a), align_bytes=64)
+                wc = const.tile([P, H], U32, name="w_c%d%d" % (s, a), align_bytes=64)
+                ws = const.tile([P, H], U8, name="w_s%d%d" % (s, a), align_bytes=64)
                 nc.vector.quantize_mx(
-                    out=w_c[:].bitcast(FP8X4), scales=w_s[:], in_=w_grp[a][:].rearrange("p c t -> p (c t)")
+                    out=wc[:].bitcast(FP8X4), scales=ws[:], in_=wg[:].rearrange("p c t -> p (c t)")
                 )
-                pg = psum.tile([P, PACK, L], F32, name="pg", tag="ps")
-                for t in range(PACK):
-                    cols = slice(t * P, (t + 1) * P)
-                    nc.tensor.matmul_mx(
-                        out=pg[:, t, :],
-                        lhsT=w_c[:, cols].bitcast(FP8X4),
-                        lhsT_scale=w_s[:, cols],
-                        rhs=a_c[:].bitcast(FP8X4),
-                        rhs_scale=a_s[:],
-                        start=True,
-                        stop=True,
-                    )
-                if a == 0:
-                    g = const.tile([P, PACK, L], F32, name="gjb%d" % s)
-                    nc.vector.tensor_tensor(
-                        out=g[:],
-                        in0=pg[:],
-                        in1=b_t[:, PACK * s : PACK * (s + 1)].unsqueeze(2).to_broadcast([P, PACK, L]),
-                        op=ALU.add,
-                    )
-                    gjb.append(g)
-                else:
-                    g = const.tile([P, PACK, L], F32, name="gi_t%d" % s)
-                    if s == 0:
-                        nc.scalar.copy(out=g[:], in_=pg[:])
-                    else:
-                        nc.vector.tensor_copy(out=g[:], in_=pg[:])
-                    gi_t.append(g)
+                wcs.append(wc)
+                wss.append(ws)
+            w_c.append(wcs)
+            w_s.append(wss)
 
         w2_grp = const.tile([P, OUT, PACK], BF16, name="w2_grp", align_bytes=64)
         nc.vector.tensor_copy(out=w2_grp[:], in_=w2_raw[:].rearrange("p t o -> p o t"))
@@ -175,31 +222,53 @@ def tile_stateencoder_pa_t_kernel(
         pos = {}
         ys = {}
 
-        def tanh1(r, s, jls):
+        def bank(r, s, t, halves):
+            jb, ib = divmod(r, IBS)
             if (r, s) not in xs:
                 xs[(r, s)] = xpool.tile([P, PACK, COLS], F32, name="x%d" % s)
-            x = xs[(r, s)]
-            for jl in jls:
-                j = r * JR + jl
-                for t in range(PACK):
-                    nc.scalar.activation(
-                        out=x[:, t, jl * L : (jl + 1) * L],
-                        in_=gi_t[s][:, t, :],
-                        func=AF.Tanh,
-                        bias=gjb[s][:, t, j : j + 1],
-                        scale=1.0,
-                    )
+            jt_c, jt_s = jts[(s, jb)]
+            hcols = slice(t * P, (t + 1) * P)
+            px = psx.tile([P, len(halves) * HALF], F32, name="px", tag="px")
+            for n, hf in enumerate(halves):
+                dst = px[:, n * HALF : (n + 1) * HALF]
+                cols = slice(hf * HALF, (hf + 1) * HALF)
+                nc.tensor.matmul_mx(
+                    out=dst,
+                    lhsT=w_c[s][0][:, hcols].bitcast(FP8X4),
+                    lhsT_scale=w_s[s][0][:, hcols],
+                    rhs=jt_c[:, cols].bitcast(FP8X4),
+                    rhs_scale=jt_s[:, cols],
+                    start=True,
+                    stop=False,
+                )
+                nc.tensor.matmul_mx(
+                    out=dst,
+                    lhsT=w_c[s][1][:, hcols].bitcast(FP8X4),
+                    lhsT_scale=w_s[s][1][:, hcols],
+                    rhs=it_c[s][:, ib, :].bitcast(FP8X4),
+                    rhs_scale=it_s[s][:, ib, :],
+                    start=False,
+                    stop=True,
+                )
+            lo = halves[0] * HALF
+            nc.scalar.activation(
+                out=xs[(r, s)][:, t, lo : lo + len(halves) * HALF],
+                in_=px[:],
+                func=AF.Tanh,
+                bias=b_t[:, PACK * s + t : PACK * s + t + 1],
+                scale=1.0,
+            )
 
         def mix(r, lo, hi):
             if r not in grps:
                 grps[r] = gpool.tile([P, COLS, PACK], BF16, name="grp", align_bytes=64)
-            x0 = xs[(r, 0)][:, :, lo * L : hi * L]
-            x1 = xs[(r, 1)][:, :, lo * L : hi * L]
+            x0 = xs[(r, 0)][:, :, lo * P : hi * P]
+            x1 = xs[(r, 1)][:, :, lo * P : hi * P]
             nc.vector.scalar_tensor_tensor(
                 out=x1, in0=x0, scalar=rho[:, 0:1], in1=x1, op0=ALU.mult, op1=ALU.add
             )
             nc.vector.tensor_scalar(
-                out=grps[r][:, lo * L : hi * L, :].rearrange("p (c i) t -> p c t i", i=4),
+                out=grps[r][:, lo * P : hi * P, :].rearrange("p (c i) t -> p c t i", i=4),
                 in0=x1.rearrange("p t (c i) -> p c t i", i=4),
                 scalar1=kap[:, 0:1],
                 scalar2=None,
@@ -213,19 +282,19 @@ def tile_stateencoder_pa_t_kernel(
                 codes[r] = (s_c, s_s)
             s_c, s_s = codes[r]
             nc.vector.quantize_mx(
-                out=s_c[:, lo * L : hi * L].bitcast(FP8X4),
-                scales=s_s[:, lo * L : hi * L],
-                in_=grps[r][:, lo * L : hi * L, :].rearrange("p c t -> p (c t)"),
+                out=s_c[:, lo * P : hi * P].bitcast(FP8X4),
+                scales=s_s[:, lo * P : hi * P],
+                in_=grps[r][:, lo * P : hi * P, :].rearrange("p c t -> p (c t)"),
             )
 
         def stage2(r, lo, hi):
             if r not in pos:
-                pos[r] = psum.tile([P, JR, OUT], F32, name="po", tag="ps")
+                pos[r] = pso.tile([P, NG, OUT], F32, name="po", tag="po")
             s_c, s_s = codes[r]
-            for jl in range(lo, hi):
-                cols = slice(jl * L, (jl + 1) * L)
+            for g in range(lo, hi):
+                cols = slice(g * P, (g + 1) * P)
                 nc.tensor.matmul_mx(
-                    out=pos[r][:, jl, :],
+                    out=pos[r][:, g, :],
                     lhsT=s_c[:, cols].bitcast(FP8X4),
                     lhsT_scale=s_s[:, cols],
                     rhs=w2_c[:].bitcast(FP8X4),
@@ -236,7 +305,7 @@ def tile_stateencoder_pa_t_kernel(
 
         def add_b2(r, lo, hi):
             if r not in ys:
-                ys[r] = ypool.tile([P, JR, OUT], F32, name="y")
+                ys[r] = ypool.tile([P, NG, OUT], F32, name="y")
             nc.vector.tensor_tensor(
                 out=ys[r][:, lo:hi, :],
                 in0=pos[r][:, lo:hi, :],
@@ -245,43 +314,55 @@ def tile_stateencoder_pa_t_kernel(
             )
 
         def tanh2_store(r, lo, hi):
+            jb, ib = divmod(r, IBS)
             y = ys[r][:, lo:hi, :]
             nc.scalar.activation(out=y, in_=y, func=AF.Tanh)
-            nc.sync.dma_start(out=out_rows[:, r * JR + lo : r * JR + hi, :], in_=y)
+            for q in range(NQ):
+                j0 = jb * NJ + q * NG
+                nc.sync.dma_start(
+                    out=out_rows[ib * NI : (ib + 1) * NI, j0 + lo : j0 + hi, :],
+                    in_=ys[r][q * NI : (q + 1) * NI, lo:hi, :],
+                )
 
         LAST = ROUNDS - 1
+        BOTH = (0, 1)
         with tc.manual_schedule():
-            tanh1(0, 0, range(JR))
-            tanh1(1, 0, range(JR))
-            tanh1(0, 1, range(JR))
-            mix(0, 0, JR)
-            tanh1(1, 1, range(JR))
-            quant(0, 0, JR)
-            stage2(0, 0, JR)
+            for s in range(2):
+                for r in range(2):
+                    for t in range(PACK):
+                        bank(r, s, t, BOTH)
+                    if s == 1 and r == 0:
+                        mix(0, 0, NG)
+            quant(0, 0, NG)
             for r in range(2, LAST):
-                tanh1(r, 0, range(JR))
-                mix(r - 1, 0, JR)
-                add_b2(r - 2, 0, JR)
-                quant(r - 1, 0, JR)
-                stage2(r - 1, 0, JR)
-                tanh1(r, 1, range(JR))
+                for k in range(2 * PACK):
+                    bank(r, k // PACK, k % PACK, BOTH)
+                    if k == STAGE2_AFTER_BANK:
+                        stage2(r - 2, 0, NG)
+                mix(r - 1, 0, NG)
+                add_b2(r - 2, 0, NG)
+                quant(r - 1, 0, NG)
+                if r % IBS >= 2 and r // IBS + 1 < JBS:
+                    build_j(r % IBS - 2, r // IBS + 1)
                 if r - 2 < FIRST_HELD:
-                    tanh2_store(r - 2, 0, JR)
+                    tanh2_store(r - 2, 0, NG)
             r = LAST
-            tanh1(r, 0, range(0, 2))
-            tanh1(r, 1, range(0, 2))
-            mix(r - 1, 0, JR)
-            add_b2(r - 2, 0, JR)
-            quant(r - 1, 0, JR)
-            stage2(r - 1, 0, JR)
-            tanh1(r, 0, range(2, 4))
-            tanh1(r, 1, range(2, 4))
+            for k in range(2 * PACK):
+                bank(r, k // PACK, k % PACK, (0,))
+                if k == STAGE2_AFTER_BANK:
+                    stage2(r - 2, 0, NG)
+            mix(r - 1, 0, NG)
+            add_b2(r - 2, 0, NG)
+            quant(r - 1, 0, NG)
+            for k in range(2 * PACK):
+                bank(r, k // PACK, k % PACK, (1,))
+            stage2(r - 1, 0, NG)
             mix(r, 0, 2)
-            add_b2(r - 1, 0, JR)
+            add_b2(r - 1, 0, NG)
             quant(r, 0, 2)
             stage2(r, 0, 2)
             for m in range(FIRST_HELD, LAST):
-                tanh2_store(m, 0, JR)
+                tanh2_store(m, 0, NG)
             mix(r, 2, 4)
             add_b2(r, 0, 2)
             quant(r, 2, 4)

@@ -49,8 +49,8 @@ def tile_stateencoder_pa_t_kernel(
         gpool = ctx.enter_context(tc.tile_pool(name="gpool", bufs=2))
         qpool = ctx.enter_context(tc.tile_pool(name="qpool", bufs=3))
         ypool = ctx.enter_context(tc.tile_pool(name="ypool", bufs=8))
-        psx = ctx.enter_context(tc.psum_pool(name="psx", bufs=6))
-        pso = ctx.enter_context(tc.psum_pool(name="pso", bufs=2))
+        psx = ctx.enter_context(tc.psum_pool(name="psx", bufs=7))
+        pso = ctx.enter_context(tc.psum_pool(name="pso", bufs=1))
 
         warm = const.tile([P, 1], F32, name="warm")
         nc.vector.memset(warm[:], 0.0)
@@ -259,21 +259,29 @@ def tile_stateencoder_pa_t_kernel(
                 scale=1.0,
             )
 
-        def mix(r, lo, hi):
-            if r not in grps:
-                grps[r] = gpool.tile([P, COLS, PACK], BF16, name="grp", align_bytes=64)
+        def mix_add(r, lo, hi):
             x0 = xs[(r, 0)][:, :, lo * P : hi * P]
             x1 = xs[(r, 1)][:, :, lo * P : hi * P]
             nc.vector.scalar_tensor_tensor(
                 out=x1, in0=x0, scalar=rho[:, 0:1], in1=x1, op0=ALU.mult, op1=ALU.add
             )
+
+        def mix_scale(r, lo, hi):
+            if r not in grps:
+                grps[r] = gpool.tile([P, COLS, PACK], BF16, name="grp", align_bytes=64)
             nc.vector.tensor_scalar(
                 out=grps[r][:, lo * P : hi * P, :].rearrange("p (c i) t -> p c t i", i=4),
-                in0=x1.rearrange("p t (c i) -> p c t i", i=4),
+                in0=xs[(r, 1)][:, :, lo * P : hi * P].rearrange("p t (c i) -> p c t i", i=4),
                 scalar1=kap[:, 0:1],
                 scalar2=None,
                 op0=ALU.mult,
             )
+
+        def mix(r):
+            mix_add(r, 0, 2)
+            mix_add(r, 2, 4)
+            mix_scale(r, 0, 2)
+            mix_scale(r, 2, 4)
 
         def quant(r, lo, hi):
             if r not in codes:
@@ -332,18 +340,19 @@ def tile_stateencoder_pa_t_kernel(
                     for t in range(PACK):
                         bank(r, s, t, BOTH)
                     if s == 1 and r == 0:
-                        mix(0, 0, NG)
+                        mix(0)
+            build_j(0, 1)
             quant(0, 0, NG)
             for r in range(2, LAST):
                 for k in range(2 * PACK):
                     bank(r, k // PACK, k % PACK, BOTH)
                     if k == STAGE2_AFTER_BANK:
                         stage2(r - 2, 0, NG)
-                mix(r - 1, 0, NG)
+                mix(r - 1)
                 add_b2(r - 2, 0, NG)
                 quant(r - 1, 0, NG)
-                if r % IBS >= 2 and r // IBS + 1 < JBS:
-                    build_j(r % IBS - 2, r // IBS + 1)
+                if r % IBS in (1, 2) and r // IBS + 1 < JBS:
+                    build_j(r % IBS - 1, r // IBS + 1)
                 if r - 2 < FIRST_HELD:
                     tanh2_store(r - 2, 0, NG)
             r = LAST
@@ -351,19 +360,21 @@ def tile_stateencoder_pa_t_kernel(
                 bank(r, k // PACK, k % PACK, (0,))
                 if k == STAGE2_AFTER_BANK:
                     stage2(r - 2, 0, NG)
-            mix(r - 1, 0, NG)
+            mix(r - 1)
             add_b2(r - 2, 0, NG)
             quant(r - 1, 0, NG)
             for k in range(2 * PACK):
                 bank(r, k // PACK, k % PACK, (1,))
             stage2(r - 1, 0, NG)
-            mix(r, 0, 2)
+            mix_add(r, 0, 2)
             add_b2(r - 1, 0, NG)
-            quant(r, 0, 2)
-            stage2(r, 0, 2)
+            mix_scale(r, 0, 2)
             for m in range(FIRST_HELD, LAST):
                 tanh2_store(m, 0, NG)
-            mix(r, 2, 4)
+            mix_add(r, 2, 4)
+            quant(r, 0, 2)
+            stage2(r, 0, 2)
+            mix_scale(r, 2, 4)
             add_b2(r, 0, 2)
             quant(r, 2, 4)
             stage2(r, 2, 4)

@@ -67,7 +67,7 @@ def tile_stateencoder_pa_t_kernel(
         a_s = []
         a_s4 = []
         for s in range(2):
-            pl = const.tile([P, L], U8, name="a_s%d" % s, align_bytes=64)
+            pl = const.tile([P, L], U8, name="a_sj%d" % s, align_bytes=64)
             nc.vector.memset(pl[:].bitcast(I32), 0)
             a_s.append(pl)
             pl4 = const.tile([P, PACK * L], U8, name="a_s4%d" % s, align_bytes=64)
@@ -130,22 +130,20 @@ def tile_stateencoder_pa_t_kernel(
         def build_j(s, jb):
             jt_c = jpool.tile([P, COLS], U32, name="jt_c%d" % s, align_bytes=64)
             jt_s = jpool.tile([P, COLS], U8, name="jt_s%d" % s, align_bytes=64)
-            js = slice(jb * NJ, (jb + 1) * NJ)
             nc.vector.tensor_copy(
-                out=jt_c[:].bitcast(I32).rearrange("p (g q l) -> p g q l", g=NG, q=NQ),
+                out=jt_c[:].bitcast(I32).rearrange("p (g l q) -> p g l q", g=NG, q=NQ),
                 in_=a_c[s][:]
-                .bitcast(I32)[:, js]
-                .rearrange("p (q g) -> p g q", g=NG)
-                .unsqueeze(3)
-                .to_broadcast([P, NG, NQ, NI]),
+                .bitcast(I32)[:, jb * NJ : (jb + 1) * NJ]
+                .rearrange("p (g q) -> p g q", g=NG)
+                .unsqueeze(2)
+                .to_broadcast([P, NG, NI, NQ]),
             )
             nc.vector.tensor_copy(
-                out=jt_s[:].bitcast(I32).rearrange("p (g q w) -> p g q w", g=NG, q=NQ),
-                in_=a_s4[s][:]
-                .bitcast(I32)[:, js]
-                .rearrange("p (q g) -> p g q", g=NG)
-                .unsqueeze(3)
-                .to_broadcast([P, NG, NQ, NI // 4]),
+                out=jt_s[:].bitcast(I32).rearrange("p (g l) -> p g l", g=NG),
+                in_=a_s[s][:]
+                .bitcast(I32)[:, jb * NG : (jb + 1) * NG]
+                .unsqueeze(2)
+                .to_broadcast([P, NG, NI]),
             )
             jts[(s, jb)] = (jt_c, jt_s)
 
@@ -160,9 +158,14 @@ def tile_stateencoder_pa_t_kernel(
                 out=a_grp4[:],
                 in_=a_grp[:].unsqueeze(2).to_broadcast([P, L, PACK, PACK]),
             )
+            a_grpj = const.tile([P, L, PACK], BF16, name="a_grpj%d" % s, align_bytes=64)
+            nc.vector.tensor_copy(
+                out=a_grpj[:].rearrange("p (b g q) t -> p b g q t", g=NG, q=NQ),
+                in_=a_grp[:].rearrange("p (b q g) t -> p b g q t", g=NG, q=NQ),
+            )
             ac = const.tile([P, L], U32, name="a_c%d" % s, align_bytes=64)
             nc.vector.quantize_mx(
-                out=ac[:].bitcast(FP8X4), scales=a_s[s][:], in_=a_grp[:].rearrange("p l t -> p (l t)")
+                out=ac[:].bitcast(FP8X4), scales=a_s[s][:], in_=a_grpj[:].rearrange("p l t -> p (l t)")
             )
             a_c.append(ac)
             ac4 = const.tile([P, PACK * L], U32, name="a_c4%d" % s, align_bytes=64)
@@ -172,20 +175,20 @@ def tile_stateencoder_pa_t_kernel(
             ic = const.tile([P, IBS, HALF], U32, name="it_c%d" % s, align_bytes=64)
             isc = const.tile([P, IBS, HALF], U8, name="it_s%d" % s, align_bytes=64)
             nc.vector.tensor_copy(
-                out=ic[:].bitcast(I32).rearrange("p b (r l) -> p b r l", l=NI),
-                in_=ac[:]
-                .bitcast(I32)
-                .rearrange("p (b l) -> p b l", b=IBS)
-                .unsqueeze(2)
-                .to_broadcast([P, IBS, HALF // NI, NI]),
-            )
-            nc.vector.tensor_copy(
-                out=isc[:].bitcast(I32).rearrange("p b (r w) -> p b r w", w=NI // 4),
-                in_=a_s[s][:]
+                out=ic[:].bitcast(I32).rearrange("p b (r w) -> p b r w", r=2),
+                in_=ac4[:]
                 .bitcast(I32)
                 .rearrange("p (b w) -> p b w", b=IBS)
                 .unsqueeze(2)
-                .to_broadcast([P, IBS, HALF // NI, NI // 4]),
+                .to_broadcast([P, IBS, 2, P]),
+            )
+            nc.vector.tensor_copy(
+                out=isc[:].bitcast(I32).rearrange("p b (r w) -> p b r w", r=2),
+                in_=a_s4[s][:]
+                .bitcast(I32)
+                .rearrange("p (b w) -> p b w", b=IBS)
+                .unsqueeze(2)
+                .to_broadcast([P, IBS, 2, P // 4]),
             )
             it_c.append(ic)
             it_s.append(isc)
@@ -329,21 +332,32 @@ def tile_stateencoder_pa_t_kernel(
                 j0 = jb * NJ + q * NG
                 nc.sync.dma_start(
                     out=out_rows[ib * NI : (ib + 1) * NI, j0 + lo : j0 + hi, :],
-                    in_=ys[r][q * NI : (q + 1) * NI, lo:hi, :],
+                    in_=ys[r][q:P:NQ, lo:hi, :],
                 )
 
         LAST = ROUNDS - 1
         BOTH = (0, 1)
         with tc.manual_schedule():
-            for s in range(2):
-                for r in range(2):
-                    for t in range(PACK):
-                        bank(r, s, t, BOTH)
-                    if s == 1 and r == 0:
-                        mix(0)
+            for r in range(3):
+                for t in range(PACK):
+                    bank(r, 0, t, BOTH)
+            for t in range(PACK):
+                bank(0, 1, t, BOTH)
+            mix(0)
+            for t in range(PACK):
+                bank(1, 1, t, BOTH)
             build_j(0, 1)
             quant(0, 0, NG)
-            for r in range(2, LAST):
+            mix(1)
+            for t in range(PACK):
+                bank(2, 1, t, BOTH)
+                if t == 1:
+                    stage2(0, 0, NG)
+            add_b2(0, 0, NG)
+            quant(1, 0, NG)
+            build_j(1, 1)
+            tanh2_store(0, 0, NG)
+            for r in range(3, LAST):
                 for k in range(2 * PACK):
                     bank(r, k // PACK, k % PACK, BOTH)
                     if k == STAGE2_AFTER_BANK:
@@ -351,7 +365,7 @@ def tile_stateencoder_pa_t_kernel(
                 mix(r - 1)
                 add_b2(r - 2, 0, NG)
                 quant(r - 1, 0, NG)
-                if r % IBS in (1, 2) and r // IBS + 1 < JBS:
+                if r > IBS and r % IBS in (1, 2) and r // IBS + 1 < JBS:
                     build_j(r % IBS - 1, r // IBS + 1)
                 if r - 2 < FIRST_HELD:
                     tanh2_store(r - 2, 0, NG)

@@ -67,7 +67,7 @@ def tile_stateencoder_pa_t_kernel(
         a_s = []
         a_s4 = []
         for s in range(2):
-            pl = const.tile([P, L], U8, name="a_sj%d" % s, align_bytes=64)
+            pl = const.tile([P, L], U8, name="a_s%d" % s, align_bytes=64)
             nc.vector.memset(pl[:].bitcast(I32), 0)
             a_s.append(pl)
             pl4 = const.tile([P, PACK * L], U8, name="a_s4%d" % s, align_bytes=64)
@@ -130,20 +130,22 @@ def tile_stateencoder_pa_t_kernel(
         def build_j(s, jb):
             jt_c = jpool.tile([P, COLS], U32, name="jt_c%d" % s, align_bytes=64)
             jt_s = jpool.tile([P, COLS], U8, name="jt_s%d" % s, align_bytes=64)
+            js = slice(jb * NJ, (jb + 1) * NJ)
             nc.vector.tensor_copy(
-                out=jt_c[:].bitcast(I32).rearrange("p (g l q) -> p g l q", g=NG, q=NQ),
+                out=jt_c[:].bitcast(I32).rearrange("p (g q l) -> p g q l", g=NG, q=NQ),
                 in_=a_c[s][:]
-                .bitcast(I32)[:, jb * NJ : (jb + 1) * NJ]
-                .rearrange("p (g q) -> p g q", g=NG)
-                .unsqueeze(2)
-                .to_broadcast([P, NG, NI, NQ]),
+                .bitcast(I32)[:, js]
+                .rearrange("p (q g) -> p g q", g=NG)
+                .unsqueeze(3)
+                .to_broadcast([P, NG, NQ, NI]),
             )
             nc.vector.tensor_copy(
-                out=jt_s[:].bitcast(I32).rearrange("p (g l) -> p g l", g=NG),
-                in_=a_s[s][:]
-                .bitcast(I32)[:, jb * NG : (jb + 1) * NG]
-                .unsqueeze(2)
-                .to_broadcast([P, NG, NI]),
+                out=jt_s[:].bitcast(I32).rearrange("p (g q w) -> p g q w", g=NG, q=NQ),
+                in_=a_s4[s][:]
+                .bitcast(I32)[:, js]
+                .rearrange("p (q g) -> p g q", g=NG)
+                .unsqueeze(3)
+                .to_broadcast([P, NG, NQ, NI // 4]),
             )
             jts[(s, jb)] = (jt_c, jt_s)
 
@@ -158,37 +160,32 @@ def tile_stateencoder_pa_t_kernel(
                 out=a_grp4[:],
                 in_=a_grp[:].unsqueeze(2).to_broadcast([P, L, PACK, PACK]),
             )
-            a_grpj = const.tile([P, L, PACK], BF16, name="a_grpj%d" % s, align_bytes=64)
-            nc.vector.tensor_copy(
-                out=a_grpj[:].rearrange("p (b g q) t -> p b g q t", g=NG, q=NQ),
-                in_=a_grp[:].rearrange("p (b q g) t -> p b g q t", g=NG, q=NQ),
-            )
             ac = const.tile([P, L], U32, name="a_c%d" % s, align_bytes=64)
             nc.vector.quantize_mx(
-                out=ac[:].bitcast(FP8X4), scales=a_s[s][:], in_=a_grpj[:].rearrange("p l t -> p (l t)")
+                out=ac[:].bitcast(FP8X4), scales=a_s[s][:], in_=a_grp[:].rearrange("p l t -> p (l t)")
             )
             a_c.append(ac)
             ac4 = const.tile([P, PACK * L], U32, name="a_c4%d" % s, align_bytes=64)
             nc.vector.quantize_mx(
                 out=ac4[:].bitcast(FP8X4), scales=a_s4[s][:], in_=a_grp4[:].rearrange("p l r t -> p (l r t)")
             )
-            ic = const.tile([P, IBS, HALF], U32, name="it_c%d" % s, align_bytes=64)
-            isc = const.tile([P, IBS, HALF], U8, name="it_s%d" % s, align_bytes=64)
+            ic = const.tile([P, IBS, COLS], U32, name="it_c%d" % s, align_bytes=64)
+            isc = const.tile([P, IBS, COLS], U8, name="it_s%d" % s, align_bytes=64)
             nc.vector.tensor_copy(
-                out=ic[:].bitcast(I32).rearrange("p b (r w) -> p b r w", r=2),
-                in_=ac4[:]
+                out=ic[:].bitcast(I32).rearrange("p b (r l) -> p b r l", l=NI),
+                in_=ac[:]
                 .bitcast(I32)
-                .rearrange("p (b w) -> p b w", b=IBS)
+                .rearrange("p (b l) -> p b l", b=IBS)
                 .unsqueeze(2)
-                .to_broadcast([P, IBS, 2, P]),
+                .to_broadcast([P, IBS, COLS // NI, NI]),
             )
             nc.vector.tensor_copy(
-                out=isc[:].bitcast(I32).rearrange("p b (r w) -> p b r w", r=2),
-                in_=a_s4[s][:]
+                out=isc[:].bitcast(I32).rearrange("p b (r w) -> p b r w", w=NI // 4),
+                in_=a_s[s][:]
                 .bitcast(I32)
                 .rearrange("p (b w) -> p b w", b=IBS)
                 .unsqueeze(2)
-                .to_broadcast([P, IBS, 2, P // 4]),
+                .to_broadcast([P, IBS, COLS // NI, NI // 4]),
             )
             it_c.append(ic)
             it_s.append(isc)
@@ -231,28 +228,27 @@ def tile_stateencoder_pa_t_kernel(
                 xs[(r, s)] = xpool.tile([P, PACK, COLS], F32, name="x%d" % s)
             jt_c, jt_s = jts[(s, jb)]
             hcols = slice(t * P, (t + 1) * P)
-            px = psx.tile([P, len(halves) * HALF], F32, name="px", tag="px")
-            for n, hf in enumerate(halves):
-                dst = px[:, n * HALF : (n + 1) * HALF]
-                cols = slice(hf * HALF, (hf + 1) * HALF)
-                nc.tensor.matmul_mx(
-                    out=dst,
-                    lhsT=w_c[s][0][:, hcols].bitcast(FP8X4),
-                    lhsT_scale=w_s[s][0][:, hcols],
-                    rhs=jt_c[:, cols].bitcast(FP8X4),
-                    rhs_scale=jt_s[:, cols],
-                    start=True,
-                    stop=False,
-                )
-                nc.tensor.matmul_mx(
-                    out=dst,
-                    lhsT=w_c[s][1][:, hcols].bitcast(FP8X4),
-                    lhsT_scale=w_s[s][1][:, hcols],
-                    rhs=it_c[s][:, ib, :].bitcast(FP8X4),
-                    rhs_scale=it_s[s][:, ib, :],
-                    start=False,
-                    stop=True,
-                )
+            width = len(halves) * HALF
+            px = psx.tile([P, width], F32, name="px", tag="px")
+            cols = slice(halves[0] * HALF, halves[0] * HALF + width)
+            nc.tensor.matmul_mx(
+                out=px[:],
+                lhsT=w_c[s][0][:, hcols].bitcast(FP8X4),
+                lhsT_scale=w_s[s][0][:, hcols],
+                rhs=jt_c[:, cols].bitcast(FP8X4),
+                rhs_scale=jt_s[:, cols],
+                start=True,
+                stop=False,
+            )
+            nc.tensor.matmul_mx(
+                out=px[:],
+                lhsT=w_c[s][1][:, hcols].bitcast(FP8X4),
+                lhsT_scale=w_s[s][1][:, hcols],
+                rhs=it_c[s][:, ib, 0:width].bitcast(FP8X4),
+                rhs_scale=it_s[s][:, ib, 0:width],
+                start=False,
+                stop=True,
+            )
             lo = halves[0] * HALF
             nc.scalar.activation(
                 out=xs[(r, s)][:, t, lo : lo + len(halves) * HALF],
@@ -332,32 +328,21 @@ def tile_stateencoder_pa_t_kernel(
                 j0 = jb * NJ + q * NG
                 nc.sync.dma_start(
                     out=out_rows[ib * NI : (ib + 1) * NI, j0 + lo : j0 + hi, :],
-                    in_=ys[r][q:P:NQ, lo:hi, :],
+                    in_=ys[r][q * NI : (q + 1) * NI, lo:hi, :],
                 )
 
         LAST = ROUNDS - 1
         BOTH = (0, 1)
         with tc.manual_schedule():
-            for r in range(3):
-                for t in range(PACK):
-                    bank(r, 0, t, BOTH)
-            for t in range(PACK):
-                bank(0, 1, t, BOTH)
-            mix(0)
-            for t in range(PACK):
-                bank(1, 1, t, BOTH)
+            for s in range(2):
+                for r in range(2):
+                    for t in range(PACK):
+                        bank(r, s, t, BOTH)
+                    if s == 1 and r == 0:
+                        mix(0)
             build_j(0, 1)
             quant(0, 0, NG)
-            mix(1)
-            for t in range(PACK):
-                bank(2, 1, t, BOTH)
-                if t == 1:
-                    stage2(0, 0, NG)
-            add_b2(0, 0, NG)
-            quant(1, 0, NG)
-            build_j(1, 1)
-            tanh2_store(0, 0, NG)
-            for r in range(3, LAST):
+            for r in range(2, LAST):
                 for k in range(2 * PACK):
                     bank(r, k // PACK, k % PACK, BOTH)
                     if k == STAGE2_AFTER_BANK:
@@ -365,7 +350,7 @@ def tile_stateencoder_pa_t_kernel(
                 mix(r - 1)
                 add_b2(r - 2, 0, NG)
                 quant(r - 1, 0, NG)
-                if r > IBS and r % IBS in (1, 2) and r // IBS + 1 < JBS:
+                if r % IBS in (1, 2) and r // IBS + 1 < JBS:
                     build_j(r % IBS - 1, r // IBS + 1)
                 if r - 2 < FIRST_HELD:
                     tanh2_store(r - 2, 0, NG)

@@ -24,11 +24,10 @@ NG = 4
 NQ = NJ // NG
 IBS = L // NI
 JBS = L // NJ
-ROUNDS = IBS * JBS
 COLS = NI * NJ
+ROUNDS = IBS * JBS
 HALF = COLS // 2
-FIRST_HELD = ROUNDS - 6
-STAGE2_AFTER_BANK = 3
+LAST = ROUNDS - 1
 RHO_MAX = 2.0**60
 
 FLOPS = 4 * 2 * L * D * H + 2 * L * L * H * OUT
@@ -44,24 +43,50 @@ def tile_stateencoder_pa_t_kernel(
 
     with ExitStack() as ctx:
         const = ctx.enter_context(tc.tile_pool(name="const", bufs=1))
-        jpool = ctx.enter_context(tc.tile_pool(name="jpool", bufs=2))
-        xpool = ctx.enter_context(tc.tile_pool(name="xpool", bufs=3))
-        gpool = ctx.enter_context(tc.tile_pool(name="gpool", bufs=2))
-        qpool = ctx.enter_context(tc.tile_pool(name="qpool", bufs=3))
-        ypool = ctx.enter_context(tc.tile_pool(name="ypool", bufs=8))
-        psx = ctx.enter_context(tc.psum_pool(name="psx", bufs=7))
-        pso = ctx.enter_context(tc.psum_pool(name="pso", bufs=1))
+        jpool = ctx.enter_context(tc.tile_pool(name="jpool", bufs=3))
+        xpool = ctx.enter_context(tc.tile_pool(name="xpool", bufs=4))
+        gpool = ctx.enter_context(tc.tile_pool(name="gpool", bufs=3))
+        qpool = ctx.enter_context(tc.tile_pool(name="qpool", bufs=4))
+        ypool = ctx.enter_context(tc.tile_pool(name="ypool", bufs=5))
+        psx = ctx.enter_context(tc.psum_pool(name="psx", bufs=6))
+        pso = ctx.enter_context(tc.psum_pool(name="pso", bufs=2))
+        ctx.enter_context(tc.manual_schedule())
+
+        a_sb = [const.tile([P, D], BF16, name="a_sb%d" % s) for s in range(2)]
+        w_raw = [const.tile([P, 2, PACK, H], BF16, name="w_raw%d" % s) for s in range(2)]
+        w2_raw = const.tile([P, PACK, OUT], BF16, name="w2_raw")
+        rowz = const.tile([P, 256], BF16, name="rowz")
+        brow = const.tile([P, P], BF16, name="brow")
+        nc.vector.memset(brow[:], 0.0)
+        nc.vector.memset(rowz[:], 0.0)
+
+        def load_a(s):
+            nc.sync.dma_start(out=a_sb[s][:], in_=acts[s].rearrange("b l k -> (b l) k"))
+
+        def load_w(s, a, lo, hi):
+            nc.sync.dma_start(
+                out=w_raw[s][:, a, :, lo:hi],
+                in_=weights[s][a * D : (a + 1) * D, lo:hi].rearrange("(t p) n -> p t n", t=PACK, p=P),
+            )
+
+        load_a(0)
+        load_w(0, 0, 0, 256)
+        load_w(0, 1, 0, 256)
+        nc.scalar.dma_start(out=brow[0:4, :], in_=b_utt.rearrange("(t p) -> t p", t=PACK))
+        nc.scalar.dma_start(out=brow[4:8, :], in_=b_sp.rearrange("(t p) -> t p", t=PACK))
+        load_w(0, 0, 256, 512)
+        load_w(0, 1, 256, 512)
+        load_a(1)
+        load_w(1, 0, 0, 512)
+        load_w(1, 1, 0, 512)
+        nc.sync.dma_start(out=rowz[0:1, 128:130], in_=mix_w.rearrange("(x o) -> x o", x=1))
+        nc.sync.dma_start(out=rowz[0:1, 144:145], in_=gamma.rearrange("(x o) -> x o", x=1))
+        nc.sync.dma_start(out=rowz[0:1, 0:OUT], in_=b2.rearrange("(x o) -> x o", x=1))
+        nc.sync.dma_start(out=w2_raw[:], in_=W2.rearrange("(t p) o -> p t o", t=PACK, p=P))
 
         warm = const.tile([P, 1], F32, name="warm")
         nc.vector.memset(warm[:], 0.0)
         nc.scalar.activation(out=warm[:], in_=warm[:], func=AF.Exp)
-        rowz = const.tile([P, 256], BF16, name="rowz")
-        nc.vector.memset(rowz[:], 0.0)
-        brow = const.tile([P, P], BF16, name="brow")
-        nc.vector.memset(brow[:], 0.0)
-        sel = const.tile([P, P], BF16, name="sel")
-        nc.vector.memset(sel[:], 0.0)
-        nc.vector.memset(sel[0:1, :], 1.0)
         ident = const.tile([P, P], BF16, name="ident")
         make_identity(nc, ident[:])
         a_s = []
@@ -73,61 +98,49 @@ def tile_stateencoder_pa_t_kernel(
             pl4 = const.tile([P, PACK * L], U8, name="a_s4%d" % s, align_bytes=64)
             nc.vector.memset(pl4[:].bitcast(I32), 0)
             a_s4.append(pl4)
+        sel = const.tile([P, P], BF16, name="sel")
+        nc.vector.memset(sel[:], 0.0)
+        nc.vector.memset(sel[0:1, :], 1.0)
 
-        nc.scalar.dma_start(out=brow[0:4, :], in_=b_utt.rearrange("(t p) -> t p", t=PACK))
-        nc.scalar.dma_start(out=brow[4:8, :], in_=b_sp.rearrange("(t p) -> t p", t=PACK))
-        nc.scalar.dma_start(out=rowz[0:1, 0:OUT], in_=b2.rearrange("(x o) -> x o", x=1))
-        nc.scalar.dma_start(out=rowz[0:1, 128:130], in_=mix_w.rearrange("(x o) -> x o", x=1))
-        nc.scalar.dma_start(out=rowz[0:1, 144:145], in_=gamma.rearrange("(x o) -> x o", x=1))
-
-        a_sb = []
-        w_raw = []
-        for s in range(2):
-            a_t = const.tile([P, D], BF16, name="a_sb%d" % s)
-            nc.sync.dma_start(out=a_t[:], in_=acts[s].rearrange("b l k -> (b l) k"))
-            a_sb.append(a_t)
-            w_t = const.tile([P, 2, PACK, H], BF16, name="w_raw%d" % s)
-            for a in range(2):
-                nc.sync.dma_start(
-                    out=w_t[:, a],
-                    in_=weights[s][a * D : (a + 1) * D, :].rearrange("(t p) n -> p t n", t=PACK, p=P),
-                )
-            w_raw.append(w_t)
-        w2_raw = const.tile([P, PACK, OUT], BF16, name="w2_raw")
-        nc.sync.dma_start(out=w2_raw[:], in_=W2.rearrange("(t p) o -> p t o", t=PACK, p=P))
-
-        pb = pso.tile([P, P], BF16, name="pb", tag="po")
-        nc.tensor.transpose(pb[:], brow[:], ident[:])
+        a_grp = [const.tile([P, L, PACK], BF16, name="a_grp%d" % s, align_bytes=64) for s in range(2)]
+        a_c = [const.tile([P, L], U32, name="a_c%d" % s, align_bytes=64) for s in range(2)]
+        it_c = [const.tile([P, IBS, HALF], U32, name="it_c%d" % s, align_bytes=64) for s in range(2)]
+        it_s = [const.tile([P, IBS, HALF], U8, name="it_s%d" % s, align_bytes=64) for s in range(2)]
+        wg = [[const.tile([P, H, PACK], BF16, name="wg%d%d" % (s, a), align_bytes=64) for a in range(2)] for s in range(2)]
+        w_c = [[const.tile([P, H], U32, name="w_c%d%d" % (s, a), align_bytes=64) for a in range(2)] for s in range(2)]
+        w_s = [[const.tile([P, H], U8, name="w_s%d%d" % (s, a), align_bytes=64) for a in range(2)] for s in range(2)]
         b_t = const.tile([P, 8], F32, name="b_t")
-        nc.vector.tensor_copy(out=b_t[:], in_=pb[:, 0:8])
-
-        pc = pso.tile([P, 256], F32, name="pc", tag="po")
-        nc.tensor.matmul(pc[:], lhsT=sel[:], rhs=rowz[:], start=True, stop=True)
-        b2bc = const.tile([P, OUT], F32, name="b2bc")
-        nc.vector.tensor_copy(out=b2bc[:], in_=pc[:, 0:OUT])
-        sm = const.tile([P, 32], F32, name="sm")
-        nc.vector.tensor_copy(out=sm[:], in_=pc[:, 128:160])
-        dd = const.tile([P, 1], F32, name="dd")
-        nc.vector.tensor_tensor(out=dd[:], in0=sm[:, 0:1], in1=sm[:, 1:2], op=ALU.subtract)
-        ex = const.tile([P, 1], F32, name="ex")
-        nc.scalar.activation(out=ex[:], in_=dd[:], func=AF.Exp)
-        rho = const.tile([P, 1], F32, name="rho")
-        nc.vector.tensor_scalar(out=rho[:], in0=ex[:], scalar1=RHO_MAX, scalar2=None, op0=ALU.min)
-        den = const.tile([P, 1], F32, name="den")
-        nc.vector.tensor_scalar(out=den[:], in0=rho[:], scalar1=1.0, scalar2=None, op0=ALU.add)
-        rden = const.tile([P, 1], F32, name="rden")
-        nc.vector.reciprocal(out=rden[:], in_=den[:])
-        kap = const.tile([P, 1], F32, name="kap")
-        nc.vector.tensor_tensor(out=kap[:], in0=rden[:], in1=sm[:, 16:17], op=ALU.mult)
-
-        a_c = []
-        it_c = []
-        it_s = []
-        w_c = []
-        w_s = []
         jts = {}
 
-        def build_j(s, jb):
+        def group_a(s):
+            pt = psx.tile([P, PACK, L], BF16, name="pt", tag="px")
+            for t in range(PACK):
+                nc.tensor.transpose(pt[:, t, :], a_sb[s][:, t * P : (t + 1) * P], ident[:])
+            nc.vector.tensor_copy(out=a_grp[s][:], in_=pt[:].rearrange("p t l -> p l t"))
+
+        def quant_a(s):
+            nc.vector.quantize_mx(
+                out=a_c[s][:].bitcast(FP8X4), scales=a_s[s][:], in_=a_grp[s][:].rearrange("p l t -> p (l t)")
+            )
+
+        def spread_j(s, jb):
+            js = slice(jb * NJ, (jb + 1) * NJ)
+            g4 = jpool.tile([P, NJ, PACK, PACK], BF16, name="g4", align_bytes=64)
+            nc.vector.tensor_copy(
+                out=g4[:].rearrange("p j r t -> p j (r t)").bitcast(I32).rearrange("p j (r t) -> p j r t", r=PACK),
+                in_=a_grp[s][:, js, :].bitcast(I32).unsqueeze(2).to_broadcast([P, NJ, PACK, PACK // 2]),
+            )
+            return g4
+
+        def quant_j(s, jb, g4):
+            c4 = jpool.tile([P, NJ * PACK], U32, name="c4", align_bytes=64)
+            nc.vector.quantize_mx(
+                out=c4[:].bitcast(FP8X4),
+                scales=a_s4[s][:, jb * NJ * PACK : (jb + 1) * NJ * PACK],
+                in_=g4[:].rearrange("p j r t -> p (j r t)"),
+            )
+
+        def codes_j(s, jb):
             jt_c = jpool.tile([P, COLS], U32, name="jt_c%d" % s, align_bytes=64)
             jt_s = jpool.tile([P, COLS], U8, name="jt_s%d" % s, align_bytes=64)
             js = slice(jb * NJ, (jb + 1) * NJ)
@@ -139,82 +152,64 @@ def tile_stateencoder_pa_t_kernel(
                 .unsqueeze(3)
                 .to_broadcast([P, NG, NQ, NI]),
             )
+            jts[(s, jb)] = (jt_c, jt_s)
+
+        def scales_j(s, jb):
+            js = slice(jb * NJ, (jb + 1) * NJ)
             nc.vector.tensor_copy(
-                out=jt_s[:].bitcast(I32).rearrange("p (g q w) -> p g q w", g=NG, q=NQ),
+                out=jts[(s, jb)][1][:].bitcast(I32).rearrange("p (g q w) -> p g q w", g=NG, q=NQ),
                 in_=a_s4[s][:]
                 .bitcast(I32)[:, js]
                 .rearrange("p (q g) -> p g q", g=NG)
                 .unsqueeze(3)
                 .to_broadcast([P, NG, NQ, NI // 4]),
             )
-            jts[(s, jb)] = (jt_c, jt_s)
 
-        for s in range(2):
-            pt = psx.tile([P, PACK, L], BF16, name="pt", tag="px")
-            for t in range(PACK):
-                nc.tensor.transpose(pt[:, t, :], a_sb[s][:, t * P : (t + 1) * P], ident[:])
-            a_grp = const.tile([P, L, PACK], BF16, name="a_grp%d" % s, align_bytes=64)
-            nc.vector.tensor_copy(out=a_grp[:], in_=pt[:].rearrange("p t l -> p l t"))
-            a_grp4 = const.tile([P, L, PACK, PACK], BF16, name="a_grp4%d" % s, align_bytes=64)
-            nc.scalar.copy(
-                out=a_grp4[:],
-                in_=a_grp[:].unsqueeze(2).to_broadcast([P, L, PACK, PACK]),
-            )
-            ac = const.tile([P, L], U32, name="a_c%d" % s, align_bytes=64)
-            nc.vector.quantize_mx(
-                out=ac[:].bitcast(FP8X4), scales=a_s[s][:], in_=a_grp[:].rearrange("p l t -> p (l t)")
-            )
-            a_c.append(ac)
-            ac4 = const.tile([P, PACK * L], U32, name="a_c4%d" % s, align_bytes=64)
-            nc.vector.quantize_mx(
-                out=ac4[:].bitcast(FP8X4), scales=a_s4[s][:], in_=a_grp4[:].rearrange("p l r t -> p (l r t)")
-            )
-            ic = const.tile([P, IBS, COLS], U32, name="it_c%d" % s, align_bytes=64)
-            isc = const.tile([P, IBS, COLS], U8, name="it_s%d" % s, align_bytes=64)
+        def build_j(s, jb):
+            g4 = spread_j(s, jb)
+            codes_j(s, jb)
+            quant_j(s, jb, g4)
+            return lambda: scales_j(s, jb)
+
+        def build_i(s, lo, hi):
+            n = hi - lo
+            ls = slice(lo * NI, hi * NI)
             nc.vector.tensor_copy(
-                out=ic[:].bitcast(I32).rearrange("p b (r l) -> p b r l", l=NI),
-                in_=ac[:]
-                .bitcast(I32)
-                .rearrange("p (b l) -> p b l", b=IBS)
+                out=it_c[s][:, lo:hi].bitcast(I32).rearrange("p b (r l) -> p b r l", l=NI),
+                in_=a_c[s][:]
+                .bitcast(I32)[:, ls]
+                .rearrange("p (b l) -> p b l", l=NI)
                 .unsqueeze(2)
-                .to_broadcast([P, IBS, COLS // NI, NI]),
+                .to_broadcast([P, n, HALF // NI, NI]),
             )
+
+        def build_is(s, lo, hi):
+            n = hi - lo
+            ws = slice(lo * NI // 4, hi * NI // 4)
             nc.vector.tensor_copy(
-                out=isc[:].bitcast(I32).rearrange("p b (r w) -> p b r w", w=NI // 4),
+                out=it_s[s][:, lo:hi].bitcast(I32).rearrange("p b (r w) -> p b r w", w=NI // 4),
                 in_=a_s[s][:]
-                .bitcast(I32)
-                .rearrange("p (b w) -> p b w", b=IBS)
+                .bitcast(I32)[:, ws]
+                .rearrange("p (b w) -> p b w", w=NI // 4)
                 .unsqueeze(2)
-                .to_broadcast([P, IBS, COLS // NI, NI // 4]),
+                .to_broadcast([P, n, HALF // NI, NI // 4]),
             )
-            it_c.append(ic)
-            it_s.append(isc)
-            build_j(s, 0)
-            wcs = []
-            wss = []
-            for a in range(2):
-                wg = const.tile([P, H, PACK], BF16, name="w_grp%d%d" % (s, a), align_bytes=64)
-                nc.vector.tensor_copy(
-                    out=wg[:].rearrange("p (c i) t -> p c t i", i=4),
-                    in_=w_raw[s][:, a].rearrange("p t (c i) -> p c t i", i=4),
-                )
-                wc = const.tile([P, H], U32, name="w_c%d%d" % (s, a), align_bytes=64)
-                ws = const.tile([P, H], U8, name="w_s%d%d" % (s, a), align_bytes=64)
-                nc.vector.quantize_mx(
-                    out=wc[:].bitcast(FP8X4), scales=ws[:], in_=wg[:].rearrange("p c t -> p (c t)")
-                )
-                wcs.append(wc)
-                wss.append(ws)
-            w_c.append(wcs)
-            w_s.append(wss)
 
-        w2_grp = const.tile([P, OUT, PACK], BF16, name="w2_grp", align_bytes=64)
-        nc.vector.tensor_copy(out=w2_grp[:], in_=w2_raw[:].rearrange("p t o -> p o t"))
-        w2_c = const.tile([P, OUT], U32, name="w2_c", align_bytes=64)
-        w2_s = const.tile([P, OUT], U8, name="w2_s", align_bytes=64)
-        nc.vector.quantize_mx(
-            out=w2_c[:].bitcast(FP8X4), scales=w2_s[:], in_=w2_grp[:].rearrange("p o t -> p (o t)")
-        )
+        def group_w(s, a, lo, hi, copy):
+            copy(
+                out=wg[s][a][:, lo:hi].rearrange("p (c i) t -> p c t i", i=4),
+                in_=w_raw[s][:, a, :, lo:hi].rearrange("p t (c i) -> p c t i", i=4),
+            )
+
+        def quant_w(s, a, lo, hi):
+            nc.vector.quantize_mx(
+                out=w_c[s][a][:, lo:hi].bitcast(FP8X4),
+                scales=w_s[s][a][:, lo:hi],
+                in_=wg[s][a][:, lo:hi].rearrange("p c t -> p (c t)"),
+            )
+
+        vcopy = nc.vector.tensor_copy
+        scopy = nc.scalar.copy
 
         xs = {}
         grps = {}
@@ -222,50 +217,50 @@ def tile_stateencoder_pa_t_kernel(
         pos = {}
         ys = {}
 
-        def bank(r, s, t, halves):
+        def bank(r, s, t, lo=0, hi=NG):
             jb, ib = divmod(r, IBS)
             if (r, s) not in xs:
                 xs[(r, s)] = xpool.tile([P, PACK, COLS], F32, name="x%d" % s)
             jt_c, jt_s = jts[(s, jb)]
             hcols = slice(t * P, (t + 1) * P)
-            width = len(halves) * HALF
-            px = psx.tile([P, width], F32, name="px", tag="px")
-            cols = slice(halves[0] * HALF, halves[0] * HALF + width)
-            nc.tensor.matmul_mx(
-                out=px[:],
-                lhsT=w_c[s][0][:, hcols].bitcast(FP8X4),
-                lhsT_scale=w_s[s][0][:, hcols],
-                rhs=jt_c[:, cols].bitcast(FP8X4),
-                rhs_scale=jt_s[:, cols],
-                start=True,
-                stop=False,
-            )
-            nc.tensor.matmul_mx(
-                out=px[:],
-                lhsT=w_c[s][1][:, hcols].bitcast(FP8X4),
-                lhsT_scale=w_s[s][1][:, hcols],
-                rhs=it_c[s][:, ib, 0:width].bitcast(FP8X4),
-                rhs_scale=it_s[s][:, ib, 0:width],
-                start=False,
-                stop=True,
-            )
-            lo = halves[0] * HALF
+            px = psx.tile([P, (hi - lo) * P], F32, name="px", tag="px")
+            for g in range(lo, hi, 2):
+                cols = slice(g * P, (g + 2) * P)
+                dst = slice((g - lo) * P, (g - lo + 2) * P)
+                nc.tensor.matmul_mx(
+                    out=px[:, dst],
+                    lhsT=w_c[s][0][:, hcols].bitcast(FP8X4),
+                    lhsT_scale=w_s[s][0][:, hcols],
+                    rhs=jt_c[:, cols].bitcast(FP8X4),
+                    rhs_scale=jt_s[:, cols],
+                    start=True,
+                    stop=False,
+                )
+                nc.tensor.matmul_mx(
+                    out=px[:, dst],
+                    lhsT=w_c[s][1][:, hcols].bitcast(FP8X4),
+                    lhsT_scale=w_s[s][1][:, hcols],
+                    rhs=it_c[s][:, ib, :].bitcast(FP8X4),
+                    rhs_scale=it_s[s][:, ib, :],
+                    start=False,
+                    stop=True,
+                )
             nc.scalar.activation(
-                out=xs[(r, s)][:, t, lo : lo + len(halves) * HALF],
+                out=xs[(r, s)][:, t, lo * P : hi * P],
                 in_=px[:],
                 func=AF.Tanh,
                 bias=b_t[:, PACK * s + t : PACK * s + t + 1],
                 scale=1.0,
             )
 
-        def mix_add(r, lo, hi):
-            x0 = xs[(r, 0)][:, :, lo * P : hi * P]
-            x1 = xs[(r, 1)][:, :, lo * P : hi * P]
+        def mix_add(r, t0, t1, lo=0, hi=NG):
+            x0 = xs[(r, 0)][:, t0:t1, lo * P : hi * P]
+            x1 = xs[(r, 1)][:, t0:t1, lo * P : hi * P]
             nc.vector.scalar_tensor_tensor(
                 out=x1, in0=x0, scalar=rho[:, 0:1], in1=x1, op0=ALU.mult, op1=ALU.add
             )
 
-        def mix_scale(r, lo, hi):
+        def mix_scale(r, lo=0, hi=NG):
             if r not in grps:
                 grps[r] = gpool.tile([P, COLS, PACK], BF16, name="grp", align_bytes=64)
             nc.vector.tensor_scalar(
@@ -276,13 +271,7 @@ def tile_stateencoder_pa_t_kernel(
                 op0=ALU.mult,
             )
 
-        def mix(r):
-            mix_add(r, 0, 2)
-            mix_add(r, 2, 4)
-            mix_scale(r, 0, 2)
-            mix_scale(r, 2, 4)
-
-        def quant(r, lo, hi):
+        def quant(r, lo=0, hi=NG):
             if r not in codes:
                 s_c = qpool.tile([P, COLS], U32, name="s_c", align_bytes=64)
                 s_s = qpool.tile([P, COLS], U8, name="s_s", align_bytes=64)
@@ -294,10 +283,10 @@ def tile_stateencoder_pa_t_kernel(
                 in_=grps[r][:, lo * P : hi * P, :].rearrange("p c t -> p (c t)"),
             )
 
-        def stage2(r, lo, hi):
+        def stage2(r, lo=0, hi=NG):
+            s_c, s_s = codes[r]
             if r not in pos:
                 pos[r] = pso.tile([P, NG, OUT], F32, name="po", tag="po")
-            s_c, s_s = codes[r]
             for g in range(lo, hi):
                 cols = slice(g * P, (g + 1) * P)
                 nc.tensor.matmul_mx(
@@ -310,73 +299,163 @@ def tile_stateencoder_pa_t_kernel(
                     stop=True,
                 )
 
-        def add_b2(r, lo, hi):
-            if r not in ys:
-                ys[r] = ypool.tile([P, NG, OUT], F32, name="y")
+        def add_b2(r, lo=0, hi=NG):
+            if r // 2 not in ys:
+                ys[r // 2] = ypool.tile([P, 2, NG, OUT], F32, name="y")
             nc.vector.tensor_tensor(
-                out=ys[r][:, lo:hi, :],
+                out=ys[r // 2][:, r % 2, lo:hi, :],
                 in0=pos[r][:, lo:hi, :],
                 in1=b2bc[:].unsqueeze(1).to_broadcast([P, hi - lo, OUT]),
                 op=ALU.add,
             )
 
-        def tanh2_store(r, lo, hi):
+        def tanh2_store(r, n, queues, lo=0, hi=NG):
             jb, ib = divmod(r, IBS)
-            y = ys[r][:, lo:hi, :]
+            y = ys[r // 2][:, r % 2 : r % 2 + n, lo:hi, :]
             nc.scalar.activation(out=y, in_=y, func=AF.Tanh)
             for q in range(NQ):
                 j0 = jb * NJ + q * NG
-                nc.sync.dma_start(
-                    out=out_rows[ib * NI : (ib + 1) * NI, j0 + lo : j0 + hi, :],
-                    in_=ys[r][q * NI : (q + 1) * NI, lo:hi, :],
+                queues[q % len(queues)].dma_start(
+                    out=out_rows[ib * NI : (ib + n) * NI, j0 + lo : j0 + hi, :].rearrange(
+                        "(b l) g o -> l b (g o)", l=NI
+                    ),
+                    in_=ys[r // 2][q * NI : (q + 1) * NI, r % 2 : r % 2 + n, lo:hi, :].rearrange("p b g o -> p b (g o)"),
                 )
 
-        LAST = ROUNDS - 1
-        BOTH = (0, 1)
-        with tc.manual_schedule():
-            for s in range(2):
-                for r in range(2):
-                    for t in range(PACK):
-                        bank(r, s, t, BOTH)
-                    if s == 1 and r == 0:
-                        mix(0)
-            build_j(0, 1)
-            quant(0, 0, NG)
-            for r in range(2, LAST):
-                for k in range(2 * PACK):
-                    bank(r, k // PACK, k % PACK, BOTH)
-                    if k == STAGE2_AFTER_BANK:
-                        stage2(r - 2, 0, NG)
-                mix(r - 1)
-                add_b2(r - 2, 0, NG)
-                quant(r - 1, 0, NG)
-                if r % IBS in (1, 2) and r // IBS + 1 < JBS:
-                    build_j(r % IBS - 1, r // IBS + 1)
-                if r - 2 < FIRST_HELD:
-                    tanh2_store(r - 2, 0, NG)
-            r = LAST
-            for k in range(2 * PACK):
-                bank(r, k // PACK, k % PACK, (0,))
-                if k == STAGE2_AFTER_BANK:
-                    stage2(r - 2, 0, NG)
-            mix(r - 1)
-            add_b2(r - 2, 0, NG)
-            quant(r - 1, 0, NG)
-            for k in range(2 * PACK):
-                bank(r, k // PACK, k % PACK, (1,))
-            stage2(r - 1, 0, NG)
-            mix_add(r, 0, 2)
-            add_b2(r - 1, 0, NG)
-            mix_scale(r, 0, 2)
-            for m in range(FIRST_HELD, LAST):
-                tanh2_store(m, 0, NG)
+        def banks(r, s, t0=0, t1=PACK):
+            for t in range(t0, t1):
+                bank(r, s, t)
+
+        group_a(0)
+        pb = pso.tile([P, P], BF16, name="pb", tag="po")
+        nc.tensor.transpose(pb[:], brow[:], ident[:])
+        group_w(0, 0, 0, 256, scopy)
+        group_w(0, 1, 0, 128, scopy)
+        group_w(0, 1, 128, 256, scopy)
+        quant_a(0)
+        spread0 = spread_j(0, 0)
+        build_i(0, 0, 1)
+        quant_j(0, 0, spread0)
+        codes_j(0, 0)
+        build_is(0, 0, 1)
+        scales_j(0, 0)
+        nc.vector.tensor_copy(out=b_t[:], in_=pb[:, 0:8])
+        quant_w(0, 0, 0, 128)
+        quant_w(0, 1, 0, 128)
+        group_w(0, 0, 256, 512, scopy)
+        bank(0, 0, 0)
+        group_w(0, 1, 256, 512, vcopy)
+        quant_w(0, 0, 128, 256)
+        quant_w(0, 1, 128, 256)
+        bank(0, 0, 1)
+        quant_w(0, 0, 256, 512)
+        quant_w(0, 1, 256, 512)
+        group_a(1)
+        bank(0, 0, 2)
+        bank(0, 0, 3)
+        build_i(0, 1, 4)
+        build_is(0, 1, 4)
+        banks(1, 0)
+        quant_a(1)
+        spread1 = spread_j(1, 0)
+        build_i(1, 0, 1)
+        quant_j(1, 0, spread1)
+        codes_j(1, 0)
+        build_is(1, 0, 1)
+        scales_j(1, 0)
+        group_w(1, 0, 0, 256, vcopy)
+        group_w(1, 1, 0, 256, vcopy)
+        quant_w(1, 0, 0, 256)
+        quant_w(1, 1, 0, 256)
+        group_w(1, 0, 256, 512, vcopy)
+        group_w(1, 1, 256, 512, vcopy)
+        quant_w(1, 0, 256, 512)
+        quant_w(1, 1, 256, 512)
+        banks(2, 0)
+
+        pc = pso.tile([P, 256], F32, name="pc", tag="po")
+        nc.tensor.matmul(pc[:], lhsT=sel[:], rhs=rowz[:], start=True, stop=True)
+        b2bc = const.tile([P, OUT], F32, name="b2bc")
+        sm = const.tile([P, 32], F32, name="sm")
+        nc.vector.tensor_copy(out=sm[:], in_=pc[:, 128:160])
+        nc.vector.tensor_copy(out=b2bc[:], in_=pc[:, 0:OUT])
+        dd = const.tile([P, 1], F32, name="dd")
+        nc.vector.tensor_tensor(out=dd[:], in0=sm[:, 0:1], in1=sm[:, 1:2], op=ALU.subtract)
+        w2_grp = const.tile([P, OUT, PACK], BF16, name="w2_grp", align_bytes=64)
+        w2_c = const.tile([P, OUT], U32, name="w2_c", align_bytes=64)
+        w2_s = const.tile([P, OUT], U8, name="w2_s", align_bytes=64)
+        nc.vector.tensor_copy(out=w2_grp[:], in_=w2_raw[:].rearrange("p t o -> p o t"))
+        build_i(1, 1, 4)
+        build_is(1, 1, 4)
+        ex = const.tile([P, 1], F32, name="ex")
+        rho = const.tile([P, 1], F32, name="rho")
+        den = const.tile([P, 1], F32, name="den")
+        rden = const.tile([P, 1], F32, name="rden")
+        kap = const.tile([P, 1], F32, name="kap")
+        bank(0, 1, 0)
+        nc.scalar.activation(out=ex[:], in_=dd[:], func=AF.Exp)
+        bank(0, 1, 1)
+        nc.vector.tensor_scalar(out=rho[:], in0=ex[:], scalar1=RHO_MAX, scalar2=None, op0=ALU.min)
+        nc.vector.quantize_mx(
+            out=w2_c[:].bitcast(FP8X4), scales=w2_s[:], in_=w2_grp[:].rearrange("p o t -> p (o t)")
+        )
+        nc.vector.tensor_scalar(out=den[:], in0=rho[:], scalar1=1.0, scalar2=None, op0=ALU.add)
+        mix_add(0, 0, 2)
+        nc.vector.reciprocal(out=rden[:], in_=den[:])
+        nc.vector.tensor_tensor(out=kap[:], in0=rden[:], in1=sm[:, 16:17], op=ALU.mult)
+        banks(0, 1, 2, 4)
+        mix_add(0, 2, 4)
+
+        for r in range(1, LAST):
+            for t in (0, 2):
+                if r > 2:
+                    banks(r, 0, t, t + 2)
+                banks(r, 1, t, t + 2)
+                if t == 0:
+                    mix_scale(r - 1)
+                    mix_add(r, 0, 2)
+                    quant(r - 1)
+                    if r % IBS in (1, 2) and r // IBS + 1 < JBS:
+                        finish = build_j(r % IBS - 1, r // IBS + 1)
+                        finish()
+                    if r % 2 == 1 and r >= 5:
+                        tanh2_store(r - 5, 2, [nc.sync])
             mix_add(r, 2, 4)
-            quant(r, 0, 2)
-            stage2(r, 0, 2)
-            mix_scale(r, 2, 4)
-            add_b2(r, 0, 2)
-            quant(r, 2, 4)
-            stage2(r, 2, 4)
-            tanh2_store(r, 0, 2)
-            add_b2(r, 2, 4)
-            tanh2_store(r, 2, 4)
+            if r >= 2:
+                stage2(r - 2)
+                add_b2(r - 2)
+
+        r = LAST
+        for t in range(PACK):
+            bank(r, 0, t, 0, 2)
+            bank(r, 1, t, 0, 2)
+            if t == 1:
+                mix_scale(r - 1)
+                mix_add(r, 0, 2, 0, 2)
+                quant(r - 1)
+                stage2(r - 2)
+                tanh2_store(r - 5, 2, [nc.sync])
+        mix_add(r, 2, 4, 0, 2)
+        add_b2(r - 2)
+        mix_scale(r, 0, 2)
+        for t in range(PACK):
+            bank(r, 0, t, 2, 4)
+            bank(r, 1, t, 2, 4)
+            if t == 1:
+                mix_add(r, 0, 2, 2, 4)
+                quant(r, 0, 2)
+                stage2(r - 1)
+            if t > 1:
+                mix_add(r, t, t + 1, 2, 4)
+                if t == 2:
+                    add_b2(r - 1)
+        tanh2_store(r - 3, 2, [nc.sync])
+        stage2(r, 0, 2)
+        mix_scale(r, 2, 4)
+        add_b2(r, 0, 2)
+        quant(r, 2, 4)
+        tanh2_store(r - 1, 1, [nc.sync])
+        tanh2_store(r, 1, [nc.sync], 0, 2)
+        stage2(r, 2, 4)
+        add_b2(r, 2, 4)
+        tanh2_store(r, 1, [nc.sync, nc.scalar], 2, 4)

@@ -28,6 +28,8 @@ COLS = NI * NJ
 ROUNDS = IBS * JBS
 HALF = COLS // 2
 LAST = ROUNDS - 1
+SETTLED = 20
+SLACK = 1
 RHO_MAX = 2.0**60
 
 FLOPS = 4 * 2 * L * D * H + 2 * L * L * H * OUT
@@ -225,8 +227,10 @@ def tile_stateencoder_pa_t_kernel(
             hcols = slice(t * P, (t + 1) * P)
             px = psx.tile([P, (hi - lo) * P], F32, name="px", tag="px")
             for g in range(lo, hi, 2):
-                cols = slice(g * P, (g + 2) * P)
-                dst = slice((g - lo) * P, (g - lo + 2) * P)
+                end = min(g + 2, hi)
+                width = (end - g) * P
+                cols = slice(g * P, end * P)
+                dst = slice((g - lo) * P, (end - lo) * P)
                 nc.tensor.matmul_mx(
                     out=px[:, dst],
                     lhsT=w_c[s][0][:, hcols].bitcast(FP8X4),
@@ -240,8 +244,8 @@ def tile_stateencoder_pa_t_kernel(
                     out=px[:, dst],
                     lhsT=w_c[s][1][:, hcols].bitcast(FP8X4),
                     lhsT_scale=w_s[s][1][:, hcols],
-                    rhs=it_c[s][:, ib, :].bitcast(FP8X4),
-                    rhs_scale=it_s[s][:, ib, :],
+                    rhs=it_c[s][:, ib, 0:width].bitcast(FP8X4),
+                    rhs_scale=it_s[s][:, ib, 0:width],
                     start=False,
                     stop=True,
                 )
@@ -339,22 +343,25 @@ def tile_stateencoder_pa_t_kernel(
         codes_j(0, 0)
         build_is(0, 0, 1)
         scales_j(0, 0)
-        nc.vector.tensor_copy(out=b_t[:], in_=pb[:, 0:8])
         quant_w(0, 0, 0, 128)
         quant_w(0, 1, 0, 128)
-        group_w(0, 0, 256, 512, scopy)
+        nc.vector.tensor_copy(out=b_t[:], in_=pb[:, 0:8])
+        group_w(0, 0, 256, 384, scopy)
         bank(0, 0, 0)
-        group_w(0, 1, 256, 512, vcopy)
         quant_w(0, 0, 128, 256)
         quant_w(0, 1, 128, 256)
         bank(0, 0, 1)
-        quant_w(0, 0, 256, 512)
-        quant_w(0, 1, 256, 512)
-        group_a(1)
+        group_w(0, 1, 256, 512, vcopy)
+        quant_w(0, 0, 256, 384)
+        group_w(0, 0, 384, 512, vcopy)
+        quant_w(0, 1, 256, 384)
         bank(0, 0, 2)
-        bank(0, 0, 3)
+        quant_w(0, 0, 384, 512)
+        quant_w(0, 1, 384, 512)
         build_i(0, 1, 4)
         build_is(0, 1, 4)
+        group_a(1)
+        bank(0, 0, 3)
         banks(1, 0)
         quant_a(1)
         spread1 = spread_j(1, 0)
@@ -406,6 +413,8 @@ def tile_stateencoder_pa_t_kernel(
         banks(0, 1, 2, 4)
         mix_add(0, 2, 4)
 
+        seconds_done = 0
+        pairs_done = 0
         for r in range(1, LAST):
             for t in (0, 2):
                 if r > 2:
@@ -418,12 +427,14 @@ def tile_stateencoder_pa_t_kernel(
                     if r % IBS in (1, 2) and r // IBS + 1 < JBS:
                         finish = build_j(r % IBS - 1, r // IBS + 1)
                         finish()
-                    if r % 2 == 1 and r >= 5:
-                        tanh2_store(r - 5, 2, [nc.sync])
+                    while pairs_done + 2 + (SLACK if r < SETTLED else 0) <= r - 3:
+                        tanh2_store(pairs_done, 2, [nc.sync])
+                        pairs_done += 2
             mix_add(r, 2, 4)
-            if r >= 2:
-                stage2(r - 2)
-                add_b2(r - 2)
+            while seconds_done <= r - 2 - (SLACK if r < SETTLED else 0):
+                stage2(seconds_done)
+                add_b2(seconds_done)
+                seconds_done += 1
 
         r = LAST
         for t in range(PACK):
@@ -439,23 +450,29 @@ def tile_stateencoder_pa_t_kernel(
         add_b2(r - 2)
         mix_scale(r, 0, 2)
         for t in range(PACK):
-            bank(r, 0, t, 2, 4)
-            bank(r, 1, t, 2, 4)
+            bank(r, 0, t, 2, 3)
+            bank(r, 1, t, 2, 3)
+        mix_add(r, 0, 4, 2, 3)
+        quant(r, 0, 2)
+        for t in range(PACK):
+            bank(r, 0, t, 3, 4)
+            bank(r, 1, t, 3, 4)
             if t == 1:
-                mix_add(r, 0, 2, 2, 4)
-                quant(r, 0, 2)
                 stage2(r - 1)
-            if t > 1:
-                mix_add(r, t, t + 1, 2, 4)
-                if t == 2:
-                    add_b2(r - 1)
-        tanh2_store(r - 3, 2, [nc.sync])
+                mix_scale(r, 2, 3)
+                add_b2(r - 1)
+                mix_add(r, 0, 2, 3, 4)
+                quant(r, 2, 3)
+                tanh2_store(r - 3, 2, [nc.sync])
+        mix_add(r, 2, 4, 3, 4)
         stage2(r, 0, 2)
-        mix_scale(r, 2, 4)
-        add_b2(r, 0, 2)
-        quant(r, 2, 4)
         tanh2_store(r - 1, 1, [nc.sync])
-        tanh2_store(r, 1, [nc.sync], 0, 2)
-        stage2(r, 2, 4)
-        add_b2(r, 2, 4)
-        tanh2_store(r, 1, [nc.sync, nc.scalar], 2, 4)
+        add_b2(r, 0, 2)
+        stage2(r, 2, 3)
+        mix_scale(r, 3, 4)
+        add_b2(r, 2, 3)
+        quant(r, 3, 4)
+        tanh2_store(r, 1, [nc.sync], 0, 3)
+        stage2(r, 3, 4)
+        add_b2(r, 3, 4)
+        tanh2_store(r, 1, [nc.sync, nc.scalar], 3, 4)

@@ -30,6 +30,8 @@ HALF = COLS // 2
 LAST = ROUNDS - 1
 SETTLED = 20
 SLACK = 1
+SPLIT = 30
+HOLD = 1
 RHO_MAX = 2.0**60
 
 FLOPS = 4 * 2 * L * D * H + 2 * L * L * H * OUT
@@ -91,21 +93,15 @@ def tile_stateencoder_pa_t_kernel(
         nc.scalar.activation(out=warm[:], in_=warm[:], func=AF.Exp)
         ident = const.tile([P, P], BF16, name="ident")
         make_identity(nc, ident[:])
-        a_s = []
-        a_s4 = []
-        for s in range(2):
-            pl = const.tile([P, L], U8, name="a_s%d" % s, align_bytes=64)
-            nc.vector.memset(pl[:].bitcast(I32), 0)
-            a_s.append(pl)
-            pl4 = const.tile([P, PACK * L], U8, name="a_s4%d" % s, align_bytes=64)
-            nc.vector.memset(pl4[:].bitcast(I32), 0)
-            a_s4.append(pl4)
+        a_c = const.tile([P, 2, L], U32, name="a_c", align_bytes=64)
+        a_s = const.tile([P, 2, L], U8, name="a_s", align_bytes=64)
+        a_s4 = const.tile([P, 2, L, 4], U8, name="a_s4", align_bytes=64)
+        nc.vector.memset(a_s[:].bitcast(I32), 0)
         sel = const.tile([P, P], BF16, name="sel")
         nc.vector.memset(sel[:], 0.0)
         nc.vector.memset(sel[0:1, :], 1.0)
 
         a_grp = [const.tile([P, L, PACK], BF16, name="a_grp%d" % s, align_bytes=64) for s in range(2)]
-        a_c = [const.tile([P, L], U32, name="a_c%d" % s, align_bytes=64) for s in range(2)]
         it_c = [const.tile([P, IBS, HALF], U32, name="it_c%d" % s, align_bytes=64) for s in range(2)]
         it_s = [const.tile([P, IBS, HALF], U8, name="it_s%d" % s, align_bytes=64) for s in range(2)]
         wg = [[const.tile([P, H, PACK], BF16, name="wg%d%d" % (s, a), align_bytes=64) for a in range(2)] for s in range(2)]
@@ -122,64 +118,49 @@ def tile_stateencoder_pa_t_kernel(
 
         def quant_a(s):
             nc.vector.quantize_mx(
-                out=a_c[s][:].bitcast(FP8X4), scales=a_s[s][:], in_=a_grp[s][:].rearrange("p l t -> p (l t)")
+                out=a_c[:, s].bitcast(FP8X4), scales=a_s[:, s], in_=a_grp[s][:].rearrange("p l t -> p (l t)")
             )
 
-        def spread_j(s, jb):
+        def spread_scales(s0, s1, lo, hi):
+            for n in range(4):
+                nc.vector.tensor_copy(out=a_s4[:, s0:s1, lo:hi, n], in_=a_s[:, s0:s1, lo:hi])
+
+        def codes_j(s0, s1, jb):
+            if jb not in jts:
+                jt_c = jpool.tile([P, 2, COLS], U32, name="jt_c", align_bytes=64)
+                jt_s = jpool.tile([P, 2, COLS], U8, name="jt_s", align_bytes=64)
+                jts[jb] = (jt_c, jt_s)
             js = slice(jb * NJ, (jb + 1) * NJ)
-            g4 = jpool.tile([P, NJ, PACK, PACK], BF16, name="g4", align_bytes=64)
-            nc.vector.tensor_copy(
-                out=g4[:].rearrange("p j r t -> p j (r t)").bitcast(I32).rearrange("p j (r t) -> p j r t", r=PACK),
-                in_=a_grp[s][:, js, :].bitcast(I32).unsqueeze(2).to_broadcast([P, NJ, PACK, PACK // 2]),
-            )
-            return g4
+            for s in range(s0, s1):
+                nc.vector.tensor_copy(
+                    out=jts[jb][0][:, s].bitcast(I32).rearrange("p (g q l) -> p g q l", g=NG, q=NQ),
+                    in_=a_c[:, s, js]
+                    .bitcast(I32)
+                    .rearrange("p (q g) -> p g q", g=NG)
+                    .unsqueeze(3)
+                    .to_broadcast([P, NG, NQ, NI]),
+                )
 
-        def quant_j(s, jb, g4):
-            c4 = jpool.tile([P, NJ * PACK], U32, name="c4", align_bytes=64)
-            nc.vector.quantize_mx(
-                out=c4[:].bitcast(FP8X4),
-                scales=a_s4[s][:, jb * NJ * PACK : (jb + 1) * NJ * PACK],
-                in_=g4[:].rearrange("p j r t -> p (j r t)"),
-            )
-
-        def codes_j(s, jb):
-            jt_c = jpool.tile([P, COLS], U32, name="jt_c%d" % s, align_bytes=64)
-            jt_s = jpool.tile([P, COLS], U8, name="jt_s%d" % s, align_bytes=64)
+        def scales_j(s0, s1, jb):
             js = slice(jb * NJ, (jb + 1) * NJ)
-            nc.vector.tensor_copy(
-                out=jt_c[:].bitcast(I32).rearrange("p (g q l) -> p g q l", g=NG, q=NQ),
-                in_=a_c[s][:]
-                .bitcast(I32)[:, js]
-                .rearrange("p (q g) -> p g q", g=NG)
-                .unsqueeze(3)
-                .to_broadcast([P, NG, NQ, NI]),
-            )
-            jts[(s, jb)] = (jt_c, jt_s)
-
-        def scales_j(s, jb):
-            js = slice(jb * NJ, (jb + 1) * NJ)
-            nc.vector.tensor_copy(
-                out=jts[(s, jb)][1][:].bitcast(I32).rearrange("p (g q w) -> p g q w", g=NG, q=NQ),
-                in_=a_s4[s][:]
-                .bitcast(I32)[:, js]
-                .rearrange("p (q g) -> p g q", g=NG)
-                .unsqueeze(3)
-                .to_broadcast([P, NG, NQ, NI // 4]),
-            )
-
-        def build_j(s, jb):
-            g4 = spread_j(s, jb)
-            codes_j(s, jb)
-            quant_j(s, jb, g4)
-            return lambda: scales_j(s, jb)
+            for s in range(s0, s1):
+                nc.vector.tensor_copy(
+                    out=jts[jb][1][:, s].bitcast(I32).rearrange("p (g q w) -> p g q w", g=NG, q=NQ),
+                    in_=a_s4[:, s, js, :]
+                    .rearrange("p j n -> p (j n)")
+                    .bitcast(I32)
+                    .rearrange("p (q g) -> p g q", g=NG)
+                    .unsqueeze(3)
+                    .to_broadcast([P, NG, NQ, NI // 4]),
+                )
 
         def build_i(s, lo, hi):
             n = hi - lo
             ls = slice(lo * NI, hi * NI)
             nc.vector.tensor_copy(
                 out=it_c[s][:, lo:hi].bitcast(I32).rearrange("p b (r l) -> p b r l", l=NI),
-                in_=a_c[s][:]
-                .bitcast(I32)[:, ls]
+                in_=a_c[:, s, ls]
+                .bitcast(I32)
                 .rearrange("p (b l) -> p b l", l=NI)
                 .unsqueeze(2)
                 .to_broadcast([P, n, HALF // NI, NI]),
@@ -187,11 +168,11 @@ def tile_stateencoder_pa_t_kernel(
 
         def build_is(s, lo, hi):
             n = hi - lo
-            ws = slice(lo * NI // 4, hi * NI // 4)
+            ls = slice(lo * NI, hi * NI)
             nc.vector.tensor_copy(
                 out=it_s[s][:, lo:hi].bitcast(I32).rearrange("p b (r w) -> p b r w", w=NI // 4),
-                in_=a_s[s][:]
-                .bitcast(I32)[:, ws]
+                in_=a_s[:, s, ls]
+                .bitcast(I32)
                 .rearrange("p (b w) -> p b w", w=NI // 4)
                 .unsqueeze(2)
                 .to_broadcast([P, n, HALF // NI, NI // 4]),
@@ -223,7 +204,7 @@ def tile_stateencoder_pa_t_kernel(
             jb, ib = divmod(r, IBS)
             if (r, s) not in xs:
                 xs[(r, s)] = xpool.tile([P, PACK, COLS], F32, name="x%d" % s)
-            jt_c, jt_s = jts[(s, jb)]
+            jt_c, jt_s = jts[jb]
             hcols = slice(t * P, (t + 1) * P)
             px = psx.tile([P, (hi - lo) * P], F32, name="px", tag="px")
             for g in range(lo, hi, 2):
@@ -235,8 +216,8 @@ def tile_stateencoder_pa_t_kernel(
                     out=px[:, dst],
                     lhsT=w_c[s][0][:, hcols].bitcast(FP8X4),
                     lhsT_scale=w_s[s][0][:, hcols],
-                    rhs=jt_c[:, cols].bitcast(FP8X4),
-                    rhs_scale=jt_s[:, cols],
+                    rhs=jt_c[:, s, cols].bitcast(FP8X4),
+                    rhs_scale=jt_s[:, s, cols],
                     start=True,
                     stop=False,
                 )
@@ -337,12 +318,11 @@ def tile_stateencoder_pa_t_kernel(
         group_w(0, 1, 0, 128, scopy)
         group_w(0, 1, 128, 256, scopy)
         quant_a(0)
-        spread0 = spread_j(0, 0)
+        codes_j(0, 1, 0)
+        spread_scales(0, 1, 0, NJ)
         build_i(0, 0, 1)
-        quant_j(0, 0, spread0)
-        codes_j(0, 0)
+        scales_j(0, 1, 0)
         build_is(0, 0, 1)
-        scales_j(0, 0)
         quant_w(0, 0, 0, 128)
         quant_w(0, 1, 0, 128)
         nc.vector.tensor_copy(out=b_t[:], in_=pb[:, 0:8])
@@ -358,18 +338,19 @@ def tile_stateencoder_pa_t_kernel(
         bank(0, 0, 2)
         quant_w(0, 0, 384, 512)
         quant_w(0, 1, 384, 512)
-        build_i(0, 1, 4)
-        build_is(0, 1, 4)
+        build_i(0, 1, 2)
+        build_is(0, 1, 2)
         group_a(1)
         bank(0, 0, 3)
         banks(1, 0)
+        build_i(0, 2, 4)
+        build_is(0, 2, 4)
         quant_a(1)
-        spread1 = spread_j(1, 0)
+        codes_j(1, 2, 0)
+        spread_scales(1, 2, 0, NJ)
         build_i(1, 0, 1)
-        quant_j(1, 0, spread1)
-        codes_j(1, 0)
+        scales_j(1, 2, 0)
         build_is(1, 0, 1)
-        scales_j(1, 0)
         group_w(1, 0, 0, 256, vcopy)
         group_w(1, 1, 0, 256, vcopy)
         quant_w(1, 0, 0, 256)
@@ -392,8 +373,10 @@ def tile_stateencoder_pa_t_kernel(
         w2_c = const.tile([P, OUT], U32, name="w2_c", align_bytes=64)
         w2_s = const.tile([P, OUT], U8, name="w2_s", align_bytes=64)
         nc.vector.tensor_copy(out=w2_grp[:], in_=w2_raw[:].rearrange("p t o -> p o t"))
-        build_i(1, 1, 4)
-        build_is(1, 1, 4)
+        build_i(1, 1, 2)
+        build_is(1, 1, 2)
+        build_i(1, 2, 4)
+        build_is(1, 2, 4)
         ex = const.tile([P, 1], F32, name="ex")
         rho = const.tile([P, 1], F32, name="rho")
         den = const.tile([P, 1], F32, name="den")
@@ -411,68 +394,59 @@ def tile_stateencoder_pa_t_kernel(
         nc.vector.reciprocal(out=rden[:], in_=den[:])
         nc.vector.tensor_tensor(out=kap[:], in0=rden[:], in1=sm[:, 16:17], op=ALU.mult)
         banks(0, 1, 2, 4)
+        spread_scales(0, 2, NJ, L)
         mix_add(0, 2, 4)
+        codes_j(0, 2, 1)
 
-        seconds_done = 0
-        pairs_done = 0
-        for r in range(1, LAST):
-            for t in (0, 2):
+        pieces = [(r, 0, NG) for r in range(1, SPLIT)]
+        pieces += [(r, lo, lo + 2) for r in range(SPLIT, LAST) for lo in (0, 2)]
+        pieces += [(LAST, 0, 2), (LAST, 2, 3), (LAST, 3, 4)]
+        mixed = [(0, 0, NG)]
+        quantised = []
+        projected = []
+        stored = 0
+        for i, (r, lo, hi) in enumerate(pieces):
+            slack = SLACK if r < SETTLED else 0
+            for t in (0, 1):
                 if r > 2:
-                    banks(r, 0, t, t + 2)
-                banks(r, 1, t, t + 2)
-                if t == 0:
-                    mix_scale(r - 1)
-                    mix_add(r, 0, 2)
-                    quant(r - 1)
-                    if r % IBS in (1, 2) and r // IBS + 1 < JBS:
-                        finish = build_j(r % IBS - 1, r // IBS + 1)
-                        finish()
-                    while pairs_done + 2 + (SLACK if r < SETTLED else 0) <= r - 3:
-                        tanh2_store(pairs_done, 2, [nc.sync])
-                        pairs_done += 2
-            mix_add(r, 2, 4)
-            while seconds_done <= r - 2 - (SLACK if r < SETTLED else 0):
-                stage2(seconds_done)
-                add_b2(seconds_done)
-                seconds_done += 1
+                    bank(r, 0, t, lo, hi)
+                bank(r, 1, t, lo, hi)
+            before = mixed[-1]
+            mix_scale(*before)
+            mix_add(r, 0, 2, lo, hi)
+            quant(*before)
+            quantised.append(before)
+            if r % IBS == 1 and r // IBS + 1 < JBS and lo == 0:
+                if r > 1:
+                    codes_j(0, 2, r // IBS + 1)
+                scales_j(0, 2, r // IBS + 1)
+            while (stored + 1, NG) in [(p[0], p[2]) for p in projected[: len(projected) - HOLD]]:
+                tanh2_store(stored, 2, [nc.sync])
+                stored += 2
+            for t in (2, 3):
+                if r > 2:
+                    bank(r, 0, t, lo, hi)
+                bank(r, 1, t, lo, hi)
+            mix_add(r, 2, 4, lo, hi)
+            mixed.append((r, lo, hi))
+            while len(projected) < len(quantised) - 1 - slack:
+                p = quantised[len(projected)]
+                stage2(*p)
+                add_b2(*p)
+                projected.append(p)
 
-        r = LAST
-        for t in range(PACK):
-            bank(r, 0, t, 0, 2)
-            bank(r, 1, t, 0, 2)
-            if t == 1:
-                mix_scale(r - 1)
-                mix_add(r, 0, 2, 0, 2)
-                quant(r - 1)
-                stage2(r - 2)
-                tanh2_store(r - 5, 2, [nc.sync])
-        mix_add(r, 2, 4, 0, 2)
-        add_b2(r - 2)
-        mix_scale(r, 0, 2)
-        for t in range(PACK):
-            bank(r, 0, t, 2, 3)
-            bank(r, 1, t, 2, 3)
-        mix_add(r, 0, 4, 2, 3)
-        quant(r, 0, 2)
-        for t in range(PACK):
-            bank(r, 0, t, 3, 4)
-            bank(r, 1, t, 3, 4)
-            if t == 1:
-                stage2(r - 1)
-                mix_scale(r, 2, 3)
-                add_b2(r - 1)
-                mix_add(r, 0, 2, 3, 4)
-                quant(r, 2, 3)
-                tanh2_store(r - 3, 2, [nc.sync])
-        mix_add(r, 2, 4, 3, 4)
-        stage2(r, 0, 2)
-        tanh2_store(r - 1, 1, [nc.sync])
-        add_b2(r, 0, 2)
-        stage2(r, 2, 3)
-        mix_scale(r, 3, 4)
-        add_b2(r, 2, 3)
-        quant(r, 3, 4)
-        tanh2_store(r, 1, [nc.sync], 0, 3)
-        stage2(r, 3, 4)
-        add_b2(r, 3, 4)
-        tanh2_store(r, 1, [nc.sync, nc.scalar], 3, 4)
+        last = pieces[-1]
+        rest = quantised[len(projected) :]
+        mix_scale(*last)
+        for p in rest:
+            stage2(*p)
+            add_b2(*p)
+        quant(*last)
+        while stored < LAST - 1:
+            tanh2_store(stored, 2, [nc.sync])
+            stored += 2
+        tanh2_store(LAST - 1, 1, [nc.sync])
+        tanh2_store(LAST, 1, [nc.sync], 0, 3)
+        stage2(*last)
+        add_b2(*last)
+        tanh2_store(LAST, 1, [nc.sync, nc.scalar], 3, 4)

@@ -61,6 +61,8 @@ def tile_stateencoder_pa_t_kernel(
         w2_raw = const.tile([P, PACK, OUT], BF16, name="w2_raw")
         rowz = const.tile([P, 256], BF16, name="rowz")
         brow = const.tile([P, P], BF16, name="brow")
+        zeros = const.tile([P, 512], BF16, name="zeros")
+        nc.gpsimd.memset(zeros[:], 0.0)
         nc.vector.memset(brow[:], 0.0)
         nc.vector.memset(rowz[:], 0.0)
 
@@ -74,8 +76,9 @@ def tile_stateencoder_pa_t_kernel(
             )
 
         load_a(0)
-        load_w(0, 0, 0, 256)
-        load_w(0, 1, 0, 256)
+        for lo in (0, 128):
+            for a in range(2):
+                load_w(0, a, lo, lo + 128)
         nc.scalar.dma_start(out=brow[0:4, :], in_=b_utt.rearrange("(t p) -> t p", t=PACK))
         nc.scalar.dma_start(out=brow[4:8, :], in_=b_sp.rearrange("(t p) -> t p", t=PACK))
         load_w(0, 0, 256, 512)
@@ -110,15 +113,21 @@ def tile_stateencoder_pa_t_kernel(
         b_t = const.tile([P, 8], F32, name="b_t")
         jts = {}
 
-        def group_a(s):
-            pt = psx.tile([P, PACK, L], BF16, name="pt", tag="px")
-            for t in range(PACK):
-                nc.tensor.transpose(pt[:, t, :], a_sb[s][:, t * P : (t + 1) * P], ident[:])
-            nc.vector.tensor_copy(out=a_grp[s][:], in_=pt[:].rearrange("p t l -> p l t"))
+        pts = {}
 
-        def quant_a(s):
+        def transpose_a(s):
+            pts[s] = psx.tile([P, PACK, L], BF16, name="pt", tag="px")
+            for t in range(PACK):
+                nc.tensor.transpose(pts[s][:, t, :], a_sb[s][:, t * P : (t + 1) * P], ident[:])
+
+        def group_a(s, lo, hi):
+            nc.vector.tensor_copy(out=a_grp[s][:, lo:hi], in_=pts[s][:, :, lo:hi].rearrange("p t l -> p l t"))
+
+        def quant_a(s, lo, hi):
             nc.vector.quantize_mx(
-                out=a_c[:, s].bitcast(FP8X4), scales=a_s[:, s], in_=a_grp[s][:].rearrange("p l t -> p (l t)")
+                out=a_c[:, s, lo:hi].bitcast(FP8X4),
+                scales=a_s[:, s, lo:hi],
+                in_=a_grp[s][:, lo:hi].rearrange("p l t -> p (l t)"),
             )
 
         def spread_scales(s0, s1, lo, hi):
@@ -311,13 +320,24 @@ def tile_stateencoder_pa_t_kernel(
             for t in range(t0, t1):
                 bank(r, s, t)
 
-        group_a(0)
+        heat = psx.tile([P, 512], F32, name="heat", tag="px")
+
+        def warm_up(count):
+            for n in range(count):
+                nc.tensor.matmul(heat[:], lhsT=zeros[:, 0:P], rhs=zeros[:], start=True, stop=True)
+
+        warm_up(2)
+        transpose_a(0)
+        group_a(0, 0, 64)
         pb = pso.tile([P, P], BF16, name="pb", tag="po")
         nc.tensor.transpose(pb[:], brow[:], ident[:])
-        group_w(0, 0, 0, 256, scopy)
+        warm_up(4)
+        group_w(0, 0, 0, 128, scopy)
         group_w(0, 1, 0, 128, scopy)
+        group_w(0, 0, 128, 256, scopy)
         group_w(0, 1, 128, 256, scopy)
-        quant_a(0)
+        group_w(0, 0, 256, 384, scopy)
+        quant_a(0, 0, 64)
         codes_j(0, 1, 0)
         spread_scales(0, 1, 0, NJ)
         build_i(0, 0, 1)
@@ -326,26 +346,29 @@ def tile_stateencoder_pa_t_kernel(
         quant_w(0, 0, 0, 128)
         quant_w(0, 1, 0, 128)
         nc.vector.tensor_copy(out=b_t[:], in_=pb[:, 0:8])
-        group_w(0, 0, 256, 384, scopy)
         bank(0, 0, 0)
+        group_w(0, 0, 384, 512, vcopy)
         quant_w(0, 0, 128, 256)
         quant_w(0, 1, 128, 256)
         bank(0, 0, 1)
-        group_w(0, 1, 256, 512, vcopy)
+        group_w(0, 1, 256, 384, vcopy)
         quant_w(0, 0, 256, 384)
-        group_w(0, 0, 384, 512, vcopy)
         quant_w(0, 1, 256, 384)
         bank(0, 0, 2)
+        group_w(0, 1, 384, 512, vcopy)
         quant_w(0, 0, 384, 512)
         quant_w(0, 1, 384, 512)
         build_i(0, 1, 2)
         build_is(0, 1, 2)
-        group_a(1)
+        group_a(0, 64, 128)
+        transpose_a(1)
         bank(0, 0, 3)
+        group_a(1, 0, L)
+        quant_a(0, 64, 128)
         banks(1, 0)
         build_i(0, 2, 4)
         build_is(0, 2, 4)
-        quant_a(1)
+        quant_a(1, 0, L)
         codes_j(1, 2, 0)
         spread_scales(1, 2, 0, NJ)
         build_i(1, 0, 1)

@@ -76,9 +76,8 @@ def tile_stateencoder_pa_t_kernel(
             )
 
         load_a(0)
-        for lo in (0, 128):
-            for a in range(2):
-                load_w(0, a, lo, lo + 128)
+        load_w(0, 0, 0, 256)
+        load_w(0, 1, 0, 256)
         nc.scalar.dma_start(out=brow[0:4, :], in_=b_utt.rearrange("(t p) -> t p", t=PACK))
         nc.scalar.dma_start(out=brow[4:8, :], in_=b_sp.rearrange("(t p) -> t p", t=PACK))
         load_w(0, 0, 256, 512)
@@ -332,9 +331,8 @@ def tile_stateencoder_pa_t_kernel(
         pb = pso.tile([P, P], BF16, name="pb", tag="po")
         nc.tensor.transpose(pb[:], brow[:], ident[:])
         warm_up(4)
-        group_w(0, 0, 0, 128, scopy)
+        group_w(0, 0, 0, 256, scopy)
         group_w(0, 1, 0, 128, scopy)
-        group_w(0, 0, 128, 256, scopy)
         group_w(0, 1, 128, 256, scopy)
         group_w(0, 0, 256, 384, scopy)
         quant_a(0, 0, 64)
@@ -406,8 +404,8 @@ def tile_stateencoder_pa_t_kernel(
         rden = const.tile([P, 1], F32, name="rden")
         kap = const.tile([P, 1], F32, name="kap")
         bank(0, 1, 0)
-        nc.scalar.activation(out=ex[:], in_=dd[:], func=AF.Exp)
         bank(0, 1, 1)
+        nc.scalar.activation(out=ex[:], in_=dd[:], func=AF.Exp)
         nc.vector.tensor_scalar(out=rho[:], in0=ex[:], scalar1=RHO_MAX, scalar2=None, op0=ALU.min)
         nc.vector.quantize_mx(
             out=w2_c[:].bitcast(FP8X4), scales=w2_s[:], in_=w2_grp[:].rearrange("p o t -> p (o t)")

@@ -30,7 +30,7 @@ HALF = COLS // 2
 LAST = ROUNDS - 1
 SETTLED = 20
 SLACK = 1
-SPLIT = 30
+SPLIT = 31
 HOLD = 1
 RHO_MAX = 2.0**60
 
@@ -61,8 +61,6 @@ def tile_stateencoder_pa_t_kernel(
         w2_raw = const.tile([P, PACK, OUT], BF16, name="w2_raw")
         rowz = const.tile([P, 256], BF16, name="rowz")
         brow = const.tile([P, P], BF16, name="brow")
-        zeros = const.tile([P, 512], BF16, name="zeros")
-        nc.gpsimd.memset(zeros[:], 0.0)
         nc.vector.memset(brow[:], 0.0)
         nc.vector.memset(rowz[:], 0.0)
 
@@ -319,18 +317,10 @@ def tile_stateencoder_pa_t_kernel(
             for t in range(t0, t1):
                 bank(r, s, t)
 
-        heat = psx.tile([P, 512], F32, name="heat", tag="px")
-
-        def warm_up(count):
-            for n in range(count):
-                nc.tensor.matmul(heat[:], lhsT=zeros[:, 0:P], rhs=zeros[:], start=True, stop=True)
-
-        warm_up(2)
         transpose_a(0)
         group_a(0, 0, 64)
         pb = pso.tile([P, P], BF16, name="pb", tag="po")
         nc.tensor.transpose(pb[:], brow[:], ident[:])
-        warm_up(4)
         group_w(0, 0, 0, 256, scopy)
         group_w(0, 1, 0, 128, scopy)
         group_w(0, 1, 128, 256, scopy)

from contextlib import ExitStack

import concourse.mybir as mybir
from concourse.masks import make_identity

F32 = mybir.dt.float32
BF16 = mybir.dt.bfloat16
U32 = mybir.dt.uint32
I32 = mybir.dt.int32
U8 = mybir.dt.uint8
FP8X4 = mybir.dt.float8_e4m3fn_x4
AF = mybir.ActivationFunctionType
ALU = mybir.AluOpType

P = 128
L = 128
D = 512
H = 512
OUT = 128
PACK = 4
NI = 32
NJ = 16
NG = 4
NQ = NJ // NG
IBS = L // NI
JBS = L // NJ
COLS = NI * NJ
ROUNDS = IBS * JBS
HALF = COLS // 2
LAST = ROUNDS - 1
SETTLED = 20
SLACK = 1
SPLIT = 31
HOLD = 1
RHO_MAX = 2.0**60

FLOPS = 4 * 2 * L * D * H + 2 * L * L * H * OUT


def tile_stateencoder_pa_t_kernel(
    tc, global_outputs, sp_outputs, W_utt, b_utt, W_sp, b_sp, W2, b2, mix_w, gamma, out
):
    nc = tc.nc
    acts = [global_outputs, sp_outputs]
    weights = [W_utt, W_sp]
    out_rows = out.rearrange("b i j o -> (b i) j o")

    with ExitStack() as ctx:
        const = ctx.enter_context(tc.tile_pool(name="const", bufs=1))
        jpool = ctx.enter_context(tc.tile_pool(name="jpool", bufs=3))
        xpool = ctx.enter_context(tc.tile_pool(name="xpool", bufs=4))
        gpool = ctx.enter_context(tc.tile_pool(name="gpool", bufs=3))
        qpool = ctx.enter_context(tc.tile_pool(name="qpool", bufs=4))
        ypool = ctx.enter_context(tc.tile_pool(name="ypool", bufs=5))
        psx = ctx.enter_context(tc.psum_pool(name="psx", bufs=6))
        pso = ctx.enter_context(tc.psum_pool(name="pso", bufs=2))
        ctx.enter_context(tc.manual_schedule())

        a_sb = [const.tile([P, D], BF16, name="a_sb%d" % s) for s in range(2)]
        w_raw = [const.tile([P, 2, PACK, H], BF16, name="w_raw%d" % s) for s in range(2)]
        w2_raw = const.tile([P, PACK, OUT], BF16, name="w2_raw")
        rowz = const.tile([P, 256], BF16, name="rowz")
        brow = const.tile([P, P], BF16, name="brow")
        nc.vector.memset(brow[:], 0.0)
        nc.vector.memset(rowz[:], 0.0)

        def load_a(s):
            nc.sync.dma_start(out=a_sb[s][:], in_=acts[s].rearrange("b l k -> (b l) k"))

        def load_w(s, a, lo, hi):
            nc.sync.dma_start(
                out=w_raw[s][:, a, :, lo:hi],
                in_=weights[s][a * D : (a + 1) * D, lo:hi].rearrange("(t p) n -> p t n", t=PACK, p=P),
            )

        load_a(0)
        load_w(0, 0, 0, 256)
        load_w(0, 1, 0, 256)
        nc.scalar.dma_start(out=brow[0:4, :], in_=b_utt.rearrange("(t p) -> t p", t=PACK))
        nc.scalar.dma_start(out=brow[4:8, :], in_=b_sp.rearrange("(t p) -> t p", t=PACK))
        load_w(0, 0, 256, 512)
        load_w(0, 1, 256, 512)
        load_a(1)
        load_w(1, 0, 0, 512)
        load_w(1, 1, 0, 512)
        nc.sync.dma_start(out=rowz[0:1, 128:130], in_=mix_w.rearrange("(x o) -> x o", x=1))
        nc.sync.dma_start(out=rowz[0:1, 144:145], in_=gamma.rearrange("(x o) -> x o", x=1))
        nc.sync.dma_start(out=rowz[0:1, 0:OUT], in_=b2.rearrange("(x o) -> x o", x=1))
        nc.sync.dma_start(out=w2_raw[:], in_=W2.rearrange("(t p) o -> p t o", t=PACK, p=P))

        warm = const.tile([P, 1], F32, name="warm")
        nc.vector.memset(warm[:], 0.0)
        nc.scalar.activation(out=warm[:], in_=warm[:], func=AF.Exp)
        ident = const.tile([P, P], BF16, name="ident")
        make_identity(nc, ident[:])
        a_c = const.tile([P, 2, L], U32, name="a_c", align_bytes=64)
        a_s = const.tile([P, 2, L], U8, name="a_s", align_bytes=64)
        a_s4 = const.tile([P, 2, L, 4], U8, name="a_s4", align_bytes=64)
        nc.vector.memset(a_s[:].bitcast(I32), 0)
        sel = const.tile([P, P], BF16, name="sel")
        nc.vector.memset(sel[:], 0.0)
        nc.vector.memset(sel[0:1, :], 1.0)

        a_grp = [const.tile([P, L, PACK], BF16, name="a_grp%d" % s, align_bytes=64) for s in range(2)]
        it_c = [const.tile([P, IBS, HALF], U32, name="it_c%d" % s, align_bytes=64) for s in range(2)]
        it_s = [const.tile([P, IBS, HALF], U8, name="it_s%d" % s, align_bytes=64) for s in range(2)]
        wg = [[const.tile([P, H, PACK], BF16, name="wg%d%d" % (s, a), align_bytes=64) for a in range(2)] for s in range(2)]
        w_c = [[const.tile([P, H], U32, name="w_c%d%d" % (s, a), align_bytes=64) for a in range(2)] for s in range(2)]
        w_s = [[const.tile([P, H], U8, name="w_s%d%d" % (s, a), align_bytes=64) for a in range(2)] for s in range(2)]
        b_t = const.tile([P, 8], F32, name="b_t")
        jts = {}

        pts = {}

        def transpose_a(s):
            pts[s] = psx.tile([P, PACK, L], BF16, name="pt", tag="px")
            for t in range(PACK):
                nc.tensor.transpose(pts[s][:, t, :], a_sb[s][:, t * P : (t + 1) * P], ident[:])

        def group_a(s, lo, hi):
            nc.vector.tensor_copy(out=a_grp[s][:, lo:hi], in_=pts[s][:, :, lo:hi].rearrange("p t l -> p l t"))

        def quant_a(s, lo, hi):
            nc.vector.quantize_mx(
                out=a_c[:, s, lo:hi].bitcast(FP8X4),
                scales=a_s[:, s, lo:hi],
                in_=a_grp[s][:, lo:hi].rearrange("p l t -> p (l t)"),
            )

        def spread_scales(s0, s1, lo, hi):
            for n in range(4):
                nc.vector.tensor_copy(out=a_s4[:, s0:s1, lo:hi, n], in_=a_s[:, s0:s1, lo:hi])

        def codes_j(s0, s1, jb):
            if jb not in jts:
                jt_c = jpool.tile([P, 2, COLS], U32, name="jt_c", align_bytes=64)
                jt_s = jpool.tile([P, 2, COLS], U8, name="jt_s", align_bytes=64)
                jts[jb] = (jt_c, jt_s)
            js = slice(jb * NJ, (jb + 1) * NJ)
            for s in range(s0, s1):
                nc.vector.tensor_copy(
                    out=jts[jb][0][:, s].bitcast(I32).rearrange("p (g q l) -> p g q l", g=NG, q=NQ),
                    in_=a_c[:, s, js]
                    .bitcast(I32)
                    .rearrange("p (q g) -> p g q", g=NG)
                    .unsqueeze(3)
                    .to_broadcast([P, NG, NQ, NI]),
                )

        def scales_j(s0, s1, jb):
            js = slice(jb * NJ, (jb + 1) * NJ)
            for s in range(s0, s1):
                nc.vector.tensor_copy(
                    out=jts[jb][1][:, s].bitcast(I32).rearrange("p (g q w) -> p g q w", g=NG, q=NQ),
                    in_=a_s4[:, s, js, :]
                    .rearrange("p j n -> p (j n)")
                    .bitcast(I32)
                    .rearrange("p (q g) -> p g q", g=NG)
                    .unsqueeze(3)
                    .to_broadcast([P, NG, NQ, NI // 4]),
                )

        def build_i(s, lo, hi):
            n = hi - lo
            ls = slice(lo * NI, hi * NI)
            nc.vector.tensor_copy(
                out=it_c[s][:, lo:hi].bitcast(I32).rearrange("p b (r l) -> p b r l", l=NI),
                in_=a_c[:, s, ls]
                .bitcast(I32)
                .rearrange("p (b l) -> p b l", l=NI)
                .unsqueeze(2)
                .to_broadcast([P, n, HALF // NI, NI]),
            )

        def build_is(s, lo, hi):
            n = hi - lo
            ls = slice(lo * NI, hi * NI)
            nc.vector.tensor_copy(
                out=it_s[s][:, lo:hi].bitcast(I32).rearrange("p b (r w) -> p b r w", w=NI // 4),
                in_=a_s[:, s, ls]
                .bitcast(I32)
                .rearrange("p (b w) -> p b w", w=NI // 4)
                .unsqueeze(2)
                .to_broadcast([P, n, HALF // NI, NI // 4]),
            )

        def group_w(s, a, lo, hi, copy):
            copy(
                out=wg[s][a][:, lo:hi].rearrange("p (c i) t -> p c t i", i=4),
                in_=w_raw[s][:, a, :, lo:hi].rearrange("p t (c i) -> p c t i", i=4),
            )

        def quant_w(s, a, lo, hi):
            nc.vector.quantize_mx(
                out=w_c[s][a][:, lo:hi].bitcast(FP8X4),
                scales=w_s[s][a][:, lo:hi],
                in_=wg[s][a][:, lo:hi].rearrange("p c t -> p (c t)"),
            )

        vcopy = nc.vector.tensor_copy
        scopy = nc.scalar.copy

        xs = {}
        grps = {}
        codes = {}
        pos = {}
        ys = {}

        def bank(r, s, t, lo=0, hi=NG):
            jb, ib = divmod(r, IBS)
            if (r, s) not in xs:
                xs[(r, s)] = xpool.tile([P, PACK, COLS], F32, name="x%d" % s)
            jt_c, jt_s = jts[jb]
            hcols = slice(t * P, (t + 1) * P)
            px = psx.tile([P, (hi - lo) * P], F32, name="px", tag="px")
            for g in range(lo, hi, 2):
                end = min(g + 2, hi)
                width = (end - g) * P
                cols = slice(g * P, end * P)
                dst = slice((g - lo) * P, (end - lo) * P)
                nc.tensor.matmul_mx(
                    out=px[:, dst],
                    lhsT=w_c[s][0][:, hcols].bitcast(FP8X4),
                    lhsT_scale=w_s[s][0][:, hcols],
                    rhs=jt_c[:, s, cols].bitcast(FP8X4),
                    rhs_scale=jt_s[:, s, cols],
                    start=True,
                    stop=False,
                )
                nc.tensor.matmul_mx(
                    out=px[:, dst],
                    lhsT=w_c[s][1][:, hcols].bitcast(FP8X4),
                    lhsT_scale=w_s[s][1][:, hcols],
                    rhs=it_c[s][:, ib, 0:width].bitcast(FP8X4),
                    rhs_scale=it_s[s][:, ib, 0:width],
                    start=False,
                    stop=True,
                )
            nc.scalar.activation(
                out=xs[(r, s)][:, t, lo * P : hi * P],
                in_=px[:],
                func=AF.Tanh,
                bias=b_t[:, PACK * s + t : PACK * s + t + 1],
                scale=1.0,
            )

        def mix_add(r, t0, t1, lo=0, hi=NG):
            x0 = xs[(r, 0)][:, t0:t1, lo * P : hi * P]
            x1 = xs[(r, 1)][:, t0:t1, lo * P : hi * P]
            nc.vector.scalar_tensor_tensor(
                out=x1, in0=x0, scalar=rho[:, 0:1], in1=x1, op0=ALU.mult, op1=ALU.add
            )

        def mix_scale(r, lo=0, hi=NG):
            if r not in grps:
                grps[r] = gpool.tile([P, COLS, PACK], BF16, name="grp", align_bytes=64)
            nc.vector.tensor_scalar(
                out=grps[r][:, lo * P : hi * P, :].rearrange("p (c i) t -> p c t i", i=4),
                in0=xs[(r, 1)][:, :, lo * P : hi * P].rearrange("p t (c i) -> p c t i", i=4),
                scalar1=kap[:, 0:1],
                scalar2=None,
                op0=ALU.mult,
            )

        def quant(r, lo=0, hi=NG):
            if r not in codes:
                s_c = qpool.tile([P, COLS], U32, name="s_c", align_bytes=64)
                s_s = qpool.tile([P, COLS], U8, name="s_s", align_bytes=64)
                codes[r] = (s_c, s_s)
            s_c, s_s = codes[r]
            nc.vector.quantize_mx(
                out=s_c[:, lo * P : hi * P].bitcast(FP8X4),
                scales=s_s[:, lo * P : hi * P],
                in_=grps[r][:, lo * P : hi * P, :].rearrange("p c t -> p (c t)"),
            )

        def stage2(r, lo=0, hi=NG):
            s_c, s_s = codes[r]
            if r not in pos:
                pos[r] = pso.tile([P, NG, OUT], F32, name="po", tag="po")
            for g in range(lo, hi):
                cols = slice(g * P, (g + 1) * P)
                nc.tensor.matmul_mx(
                    out=pos[r][:, g, :],
                    lhsT=s_c[:, cols].bitcast(FP8X4),
                    lhsT_scale=s_s[:, cols],
                    rhs=w2_c[:].bitcast(FP8X4),
                    rhs_scale=w2_s[:],
                    start=True,
                    stop=True,
                )

        def add_b2(r, lo=0, hi=NG):
            if r // 2 not in ys:
                ys[r // 2] = ypool.tile([P, 2, NG, OUT], F32, name="y")
            nc.vector.tensor_tensor(
                out=ys[r // 2][:, r % 2, lo:hi, :],
                in0=pos[r][:, lo:hi, :],
                in1=b2bc[:].unsqueeze(1).to_broadcast([P, hi - lo, OUT]),
                op=ALU.add,
            )

        def tanh2_store(r, n, queues, lo=0, hi=NG):
            jb, ib = divmod(r, IBS)
            y = ys[r // 2][:, r % 2 : r % 2 + n, lo:hi, :]
            nc.scalar.activation(out=y, in_=y, func=AF.Tanh)
            for q in range(NQ):
                j0 = jb * NJ + q * NG
                queues[q % len(queues)].dma_start(
                    out=out_rows[ib * NI : (ib + n) * NI, j0 + lo : j0 + hi, :].rearrange(
                        "(b l) g o -> l b (g o)", l=NI
                    ),
                    in_=ys[r // 2][q * NI : (q + 1) * NI, r % 2 : r % 2 + n, lo:hi, :].rearrange("p b g o -> p b (g o)"),
                )

        def banks(r, s, t0=0, t1=PACK):
            for t in range(t0, t1):
                bank(r, s, t)

        transpose_a(0)
        group_a(0, 0, 64)
        pb = pso.tile([P, P], BF16, name="pb", tag="po")
        nc.tensor.transpose(pb[:], brow[:], ident[:])
        group_w(0, 0, 0, 256, scopy)
        group_w(0, 1, 0, 128, scopy)
        group_w(0, 1, 128, 256, scopy)
        group_w(0, 0, 256, 384, scopy)
        quant_a(0, 0, 64)
        codes_j(0, 1, 0)
        spread_scales(0, 1, 0, NJ)
        build_i(0, 0, 1)
        scales_j(0, 1, 0)
        build_is(0, 0, 1)
        quant_w(0, 0, 0, 128)
        quant_w(0, 1, 0, 128)
        nc.vector.tensor_copy(out=b_t[:], in_=pb[:, 0:8])
        bank(0, 0, 0)
        group_w(0, 0, 384, 512, vcopy)
        quant_w(0, 0, 128, 256)
        quant_w(0, 1, 128, 256)
        bank(0, 0, 1)
        group_w(0, 1, 256, 384, vcopy)
        quant_w(0, 0, 256, 384)
        quant_w(0, 1, 256, 384)
        bank(0, 0, 2)
        group_w(0, 1, 384, 512, vcopy)
        quant_w(0, 0, 384, 512)
        quant_w(0, 1, 384, 512)
        build_i(0, 1, 2)
        build_is(0, 1, 2)
        group_a(0, 64, 128)
        transpose_a(1)
        bank(0, 0, 3)
        group_a(1, 0, L)
        quant_a(0, 64, 128)
        banks(1, 0)
        build_i(0, 2, 4)
        build_is(0, 2, 4)
        quant_a(1, 0, L)
        codes_j(1, 2, 0)
        spread_scales(1, 2, 0, NJ)
        build_i(1, 0, 1)
        scales_j(1, 2, 0)
        build_is(1, 0, 1)
        group_w(1, 0, 0, 256, vcopy)
        group_w(1, 1, 0, 256, vcopy)
        quant_w(1, 0, 0, 256)
        quant_w(1, 1, 0, 256)
        group_w(1, 0, 256, 512, vcopy)
        group_w(1, 1, 256, 512, vcopy)
        quant_w(1, 0, 256, 512)
        quant_w(1, 1, 256, 512)
        banks(2, 0)

        pc = pso.tile([P, 256], F32, name="pc", tag="po")
        nc.tensor.matmul(pc[:], lhsT=sel[:], rhs=rowz[:], start=True, stop=True)
        b2bc = const.tile([P, OUT], F32, name="b2bc")
        sm = const.tile([P, 32], F32, name="sm")
        nc.vector.tensor_copy(out=sm[:], in_=pc[:, 128:160])
        nc.vector.tensor_copy(out=b2bc[:], in_=pc[:, 0:OUT])
        dd = const.tile([P, 1], F32, name="dd")
        nc.vector.tensor_tensor(out=dd[:], in0=sm[:, 0:1], in1=sm[:, 1:2], op=ALU.subtract)
        w2_grp = const.tile([P, OUT, PACK], BF16, name="w2_grp", align_bytes=64)
        w2_c = const.tile([P, OUT], U32, name="w2_c", align_bytes=64)
        w2_s = const.tile([P, OUT], U8, name="w2_s", align_bytes=64)
        nc.vector.tensor_copy(out=w2_grp[:], in_=w2_raw[:].rearrange("p t o -> p o t"))
        build_i(1, 1, 2)
        build_is(1, 1, 2)
        build_i(1, 2, 4)
        build_is(1, 2, 4)
        ex = const.tile([P, 1], F32, name="ex")
        rho = const.tile([P, 1], F32, name="rho")
        den = const.tile([P, 1], F32, name="den")
        rden = const.tile([P, 1], F32, name="rden")
        kap = const.tile([P, 1], F32, name="kap")
        bank(0, 1, 0)
        bank(0, 1, 1)
        nc.scalar.activation(out=ex[:], in_=dd[:], func=AF.Exp)
        nc.vector.tensor_scalar(out=rho[:], in0=ex[:], scalar1=RHO_MAX, scalar2=None, op0=ALU.min)
        nc.vector.quantize_mx(
            out=w2_c[:].bitcast(FP8X4), scales=w2_s[:], in_=w2_grp[:].rearrange("p o t -> p (o t)")
        )
        nc.vector.tensor_scalar(out=den[:], in0=rho[:], scalar1=1.0, scalar2=None, op0=ALU.add)
        mix_add(0, 0, 2)
        nc.vector.reciprocal(out=rden[:], in_=den[:])
        nc.vector.tensor_tensor(out=kap[:], in0=rden[:], in1=sm[:, 16:17], op=ALU.mult)
        banks(0, 1, 2, 4)
        spread_scales(0, 2, NJ, L)
        mix_add(0, 2, 4)
        codes_j(0, 2, 1)

        pieces = [(r, 0, NG) for r in range(1, SPLIT)]
        pieces += [(r, lo, lo + 2) for r in range(SPLIT, LAST) for lo in (0, 2)]
        pieces += [(LAST, 0, 2), (LAST, 2, 3), (LAST, 3, 4)]
        mixed = [(0, 0, NG)]
        quantised = []
        projected = []
        stored = 0
        for i, (r, lo, hi) in enumerate(pieces):
            slack = SLACK if r < SETTLED else 0
            for t in (0, 1):
                if r > 2:
                    bank(r, 0, t, lo, hi)
                bank(r, 1, t, lo, hi)
            before = mixed[-1]
            mix_scale(*before)
            mix_add(r, 0, 2, lo, hi)
            quant(*before)
            quantised.append(before)
            if r % IBS == 1 and r // IBS + 1 < JBS and lo == 0:
                if r > 1:
                    codes_j(0, 2, r // IBS + 1)
                scales_j(0, 2, r // IBS + 1)
            while (stored + 1, NG) in [(p[0], p[2]) for p in projected[: len(projected) - HOLD]]:
                tanh2_store(stored, 2, [nc.sync])
                stored += 2
            for t in (2, 3):
                if r > 2:
                    bank(r, 0, t, lo, hi)
                bank(r, 1, t, lo, hi)
            mix_add(r, 2, 4, lo, hi)
            mixed.append((r, lo, hi))
            while len(projected) < len(quantised) - 1 - slack:
                p = quantised[len(projected)]
                stage2(*p)
                add_b2(*p)
                projected.append(p)

        last = pieces[-1]
        rest = quantised[len(projected) :]
        mix_scale(*last)
        for p in rest:
            stage2(*p)
            add_b2(*p)
        quant(*last)
        while stored < LAST - 1:
            tanh2_store(stored, 2, [nc.sync])
            stored += 2
        tanh2_store(LAST - 1, 1, [nc.sync])
        tanh2_store(LAST, 1, [nc.sync], 0, 3)
        stage2(*last)
        add_b2(*last)
        tanh2_store(LAST, 1, [nc.sync, nc.scalar], 3, 4)
